import numpy as np
import ml_dtypes


def mxq(x, axis, fmt="e4m3"):
    dtype, down = {"e4m3": (ml_dtypes.float8_e4m3fn, 7), "e5m2": (ml_dtypes.float8_e5m2, 14)}[fmt]
    v = np.moveaxis(np.asarray(x, np.float32).astype(ml_dtypes.bfloat16).astype(np.float64), axis, -1)
    blocks = v.reshape(v.shape[:-1] + (-1, 32))
    amax = np.abs(blocks).max(-1, keepdims=True)
    byte = np.maximum(np.where(amax > 0, np.frexp(amax)[1] - 1 + 127, 0) - down, 1)
    scale = np.exp2(byte - 127.0)
    codes = (blocks / scale).astype(np.float32).astype(dtype).astype(np.float64)
    return np.moveaxis((codes * scale).reshape(v.shape), -1, axis)


WIDE = False


def mx_kscale(k):
    if not WIDE:
        return np.ones(k)
    levels = np.array([10, -10, 5, -5, 0])
    if k % 512:
        return np.exp2(np.random.permutation(np.resize(levels, k // 32))).repeat(32)
    a = np.empty((k // 512, 16))
    for p in range(k // 512):
        a[p, :8] = np.random.permutation(np.resize(levels, 8))
        for g in range(8):
            far = levels[np.abs(levels - a[p, g]) >= 10]
            a[p, g + 8] = far[np.random.randint(len(far))]
    return np.exp2(a.ravel()).repeat(32)


BF16 = ml_dtypes.bfloat16


def bf(x):
    return np.asarray(x, np.float32).astype(BF16)


def f64(x):
    return np.asarray(x).astype(np.float64)


B, L, D, O = 4, 128, 512, 32


def setup_inputs():
    s = mx_kscale(D)
    u = mx_kscale(D)
    w = np.random.standard_normal((O, D + 1, D))
    w[:, :D, :] *= 3.0 / D / s[:, None]
    w[:, D, :] *= 1.0 / np.sqrt(D)
    return {"x1": bf(np.random.standard_normal((B, L, D)) * s),
            "x2": bf(np.random.standard_normal((B, L, D)) / u),
            "bw": bf(np.random.uniform(size=(2,))),
            "W_bil": bf(w * u),
            "t_ones": bf(np.random.standard_normal((B, L, O))),
            "lin1": bf(np.random.standard_normal((B, L, O))),
            "lin2": bf(np.random.standard_normal((B, L, O))),
            "b_lin": bf(np.random.standard_normal(O) * 0.5)}


def reference(x1, x2, bw, W_bil, t_ones, lin1, lin2, b_lin):
    e = np.exp(f64(bw) - f64(bw).max())
    bwn = e / e.sum()
    w = f64(W_bil)
    t = f64(bf(mxq(f64(x1).reshape(B * L, D), 1, "e4m3") @ mxq(w[:, :D, :], 1, "e4m3"))) + w[:, D, :][:, None, :]
    t = t.reshape(O, B, L, D)
    pair = mxq(t, 3, "e4m3") @ mxq(f64(x2), 2, "e4m3").transpose(0, 2, 1)
    bil = pair.transpose(1, 2, 3, 0) + f64(t_ones)[:, :, None, :]
    lin = f64(lin1)[:, :, None, :] + f64(lin2)[:, None, :, :] + f64(b_lin)
    return bwn[0] * bil + bwn[1] * lin

@@ -1,0 +1,259 @@
+from contextlib import ExitStack
+
+import concourse.mybir as mybir
+from concourse.masks import make_identity
+
+B, L, D, O = 4, 128, 512, 32
+FLOPS = 2 * B * L * D * D * O + 2 * O * B * L * L * D
+
+F32 = mybir.dt.float32
+BF16 = mybir.dt.bfloat16
+U32 = mybir.dt.uint32
+U8 = mybir.dt.uint8
+FP8X4 = mybir.dt.float8_e4m3fn_x4
+ALU = mybir.AluOpType
+ACT = mybir.ActivationFunctionType
+
+P = 128
+PACK = 4
+BANK_DT = BF16
+OGRP = 4
+YH = 64
+V_READ_EVERY = 64
+W_BUFS = 5
+MANUAL = False
+V_COPY_Q = [1]
+
+
+def tile_biaffine_pa_kernel(tc, x1, x2, bw, W_bil, t_ones, lin1, lin2, b_lin, out):
+    nc = tc.nc
+    with ExitStack() as ctx:
+        keep = ctx.enter_context(tc.tile_pool(name="keep", bufs=1))
+        work = ctx.enter_context(tc.tile_pool(name="work", bufs=2))
+        psum = ctx.enter_context(tc.psum_pool(name="psum", bufs=8))
+        if MANUAL:
+            ctx.enter_context(tc.manual_schedule())
+
+        bw_sb = keep.tile([P, 2], BF16, name="bw_sb", tag="bw_sb")
+        nc.scalar.dma_start(out=bw_sb[:], in_=bw.partition_broadcast(P))
+        bl_sb = keep.tile([P, O], BF16, name="bl_sb", tag="bl_sb")
+        nc.scalar.dma_start(out=bl_sb[:], in_=b_lin.partition_broadcast(P))
+        t1_sb = keep.tile([P, B, O], BF16, name="t1_sb", tag="t1_sb")
+        nc.scalar.dma_start(out=t1_sb[:], in_=t_ones.rearrange("b x o -> x b o"))
+        l1_sb = keep.tile([P, B, O], BF16, name="l1_sb", tag="l1_sb")
+        nc.scalar.dma_start(out=l1_sb[:], in_=lin1.rearrange("b x o -> x b o"))
+
+        ident = keep.tile([P, P], F32, name="ident", tag="ident")
+        make_identity(nc, ident[:])
+
+        x1c = keep.tile([P, B * L], U32, name="x1c", tag="x1c", align_bytes=64)
+        x1s = keep.tile([P, B * L], U8, name="x1s", tag="x1s", align_bytes=64)
+        x2c = keep.tile([P, B * L], U32, name="x2c", tag="x2c", align_bytes=64)
+        x2s = keep.tile([P, B * L], U8, name="x2s", tag="x2s", align_bytes=64)
+        tcod = keep.tile([P, O, B * L], U32, name="tcod", tag="tcod", align_bytes=64)
+        tscl = keep.tile([P, O, B * L], U8, name="tscl", tag="tscl", align_bytes=64)
+
+        wraw, wgrp, wq, banks, tbs, xts, tgs, biases, lin2bs = {}, {}, {}, {}, {}, {}, {}, {}, {}
+
+        def load_tokens(x, key):
+            raw = work.tile([P, B, D], BF16, name="xraw", tag="wraw", bufs=W_BUFS, align_bytes=64)
+            for b in range(B):
+                nc.sync.dma_start(out=raw[:, b, :], in_=x[b])
+            tbs[key] = raw
+
+        def load_w(o):
+            raw = work.tile([P, PACK, D], BF16, name="wraw", tag="wraw", bufs=W_BUFS, align_bytes=64)
+            nc.sync.dma_start(out=raw[:], in_=W_bil[o, 0:D, :].rearrange("(p s) j -> p s j", s=PACK))
+            wraw[o] = raw
+
+        def load_bias(c):
+            bt = work.tile([P, OGRP, D], BF16, name="bias", tag="bias", bufs=2)
+            nc.sync.dma_start(out=bt[:], in_=W_bil[c * OGRP : (c + 1) * OGRP, D, :].partition_broadcast(P))
+            biases[c] = bt
+
+        def load_lin2(b):
+            l2 = work.tile([P, L, O], BF16, name="lin2b", tag="lin2b", bufs=4)
+            nc.sync.dma_start(out=l2[:].rearrange("p y o -> p (y o)"), in_=lin2[b].rearrange("y o -> (y o)").partition_broadcast(P))
+            lin2bs[b] = l2
+
+        def interleave_w(o, copies):
+            g = work.tile([P, D, PACK], BF16, name="wgrp", tag="wgrp", bufs=3, align_bytes=64)
+            dst = g[:].rearrange("p (u c e) s -> p u c s e", u=2, e=2)
+            src = wraw[o][:].rearrange("p s (c u e) -> p u c s e", u=2, e=2)
+            for u in range(2):
+                copies[u](out=dst[:, u], in_=src[:, u])
+            wgrp[o] = g
+
+        def quant_w(o):
+            wc = work.tile([P, D], U32, name="wc", tag="wc", bufs=3, align_bytes=64)
+            ws = work.tile([P, D], U8, name="ws", tag="ws", bufs=3, align_bytes=64)
+            nc.vector.quantize_mx(out=wc[:].bitcast(FP8X4), scales=ws[:], in_=wgrp[o][:].rearrange("p j s -> p (j s)"))
+            wq[o] = (wc, ws)
+
+        def stage1(o):
+            wc, ws = wq[o]
+            banks[o] = []
+            for b in range(B):
+                cols = slice(b * L, (b + 1) * L)
+                bank = psum.tile([P, D], BANK_DT, name="bank", tag="bank")
+                nc.tensor.matmul_mx(
+                    out=bank[:],
+                    lhsT=x1c[:, cols].bitcast(FP8X4),
+                    lhsT_scale=x1s[:, cols],
+                    rhs=wc[:].bitcast(FP8X4),
+                    rhs_scale=ws[:],
+                    start=True,
+                    stop=True,
+                )
+                banks[o].append(bank)
+
+        def add_bias(o):
+            tb = work.tile([P, B, D], BF16, name="tb", tag="tb", bufs=2, align_bytes=64)
+            for b in range(B):
+                nc.vector.tensor_tensor(
+                    out=tb[:, b, :].rearrange("p (u c e) -> p u c e", u=2, e=2),
+                    in0=banks[o][b][:].rearrange("p (u c e) -> p u c e", u=2, e=2),
+                    in1=biases[o // OGRP][:, o % OGRP, :].rearrange("p (c u e) -> p u c e", u=2, e=2),
+                    op=ALU.add,
+                )
+            tbs[o] = tb
+
+        def transposes(key, permuted):
+            words = tbs[key][:].bitcast(F32)
+            xts[key] = []
+            for q in range(2):
+                xt = psum.tile([P, 2, 2, L], F32, name="xt", tag="bank")
+                for h in range(2):
+                    for u in range(2):
+                        if permuted:
+                            sel = words[:, 2 * q + h, u * P : (u + 1) * P]
+                        else:
+                            sel = words[:, 2 * q + h, u : D // 2 : 2]
+                        nc.tensor.transpose(xt[:, h, u, :], sel, ident[:])
+                xts[key].append(xt)
+
+        def copy_out(key, v_q):
+            tg = work.tile([P, B * L * PACK], BF16, name="tg", tag="tg", bufs=2, align_bytes=64)
+            gw = tg[:].bitcast(F32).rearrange("p (b x u) -> p b x u", b=B, u=2)
+            for q in range(2):
+                src = xts[key][q][:].rearrange("p h u x -> p h x u")
+                if q in v_q:
+                    nc.vector.tensor_copy(out=gw[:, 2 * q : 2 * q + 2], in_=src)
+                else:
+                    nc.scalar.copy(out=gw[:, 2 * q : 2 * q + 2], in_=src)
+            tgs[key] = tg
+
+        def quant_tokens(key, codes, scales):
+            nc.vector.quantize_mx(out=codes.bitcast(FP8X4), scales=scales, in_=tgs[key][:])
+
+        load_tokens(x1, "x1")
+        load_w(0)
+        load_w(1)
+        load_bias(0)
+        load_tokens(x2, "x2")
+        load_w(2)
+        load_w(3)
+
+        bwf = keep.tile([P, 2], F32, name="bwf", tag="bwf")
+        nc.vector.tensor_copy(out=bwf[:], in_=bw_sb[:])
+        bmax = keep.tile([P, 1], F32, name="bmax", tag="bmax")
+        nc.vector.tensor_tensor(out=bmax[:], in0=bwf[:, 0:1], in1=bwf[:, 1:2], op=ALU.max)
+        nmax = keep.tile([P, 1], F32, name="nmax", tag="nmax")
+        nc.vector.tensor_scalar(out=nmax[:], in0=bmax[:], scalar1=-1.0, scalar2=None, op0=ALU.mult)
+        bexp = keep.tile([P, 2], F32, name="bexp", tag="bexp")
+        nc.scalar.activation(out=bexp[:], in_=bwf[:], func=ACT.Exp, bias=nmax[:], scale=1.0)
+        bsum = keep.tile([P, 1], F32, name="bsum", tag="bsum")
+        nc.vector.tensor_tensor(out=bsum[:], in0=bexp[:, 0:1], in1=bexp[:, 1:2], op=ALU.add)
+        brec = keep.tile([P, 1], F32, name="brec", tag="brec")
+        nc.vector.reciprocal(out=brec[:], in_=bsum[:])
+        bwn = keep.tile([P, 2], F32, name="bwn", tag="bwn")
+        nc.vector.tensor_scalar(out=bwn[:], in0=bexp[:], scalar1=brec[:], scalar2=None, op0=ALU.mult)
+
+        lsum = keep.tile([P, B, O], F32, name="lsum", tag="lsum")
+        nc.vector.tensor_tensor(out=lsum[:], in0=l1_sb[:], in1=bl_sb[:].unsqueeze(1).to_broadcast([P, B, O]), op=ALU.add)
+        lscl = keep.tile([P, B * O], F32, name="lscl", tag="lscl")
+        nc.vector.tensor_scalar(out=lscl[:], in0=lsum[:].rearrange("p b o -> p (b o)"), scalar1=bwn[:, 1:2], scalar2=None, op0=ALU.mult)
+        xterm = keep.tile([P, B * O], F32, name="xterm", tag="xterm")
+        nc.vector.scalar_tensor_tensor(out=xterm[:], in0=t1_sb[:].rearrange("p b o -> p (b o)"), scalar=bwn[:, 0:1], in1=lscl[:], op0=ALU.mult, op1=ALU.add)
+
+        transposes("x1", False)
+        copy_out("x1", [1])
+        interleave_w(0, [nc.scalar.copy, nc.vector.tensor_copy])
+        quant_tokens("x1", x1c[:], x1s[:])
+        transposes("x2", False)
+        copy_out("x2", [0, 1])
+        quant_w(0)
+        interleave_w(1, [nc.scalar.copy, nc.scalar.copy])
+        quant_tokens("x2", x2c[:], x2s[:])
+        stage1(0)
+        interleave_w(2, [nc.scalar.copy, nc.scalar.copy])
+        quant_w(1)
+
+        for i in range(O + 1):
+            if 4 <= i + 4 < O:
+                load_w(i + 4)
+            if (i + 2) % OGRP == 0 and (i + 2) // OGRP < O // OGRP:
+                load_bias((i + 2) // OGRP)
+            if O - 16 <= i < O and i % 4 == 0:
+                load_lin2((i - (O - 16)) // 4)
+            if 0 <= i - 1:
+                copy_out(i - 1, V_COPY_Q)
+            if i + 3 < O:
+                interleave_w(i + 3, [nc.scalar.copy, nc.scalar.copy])
+            if i + 1 < O:
+                stage1(i + 1)
+            if i < O:
+                add_bias(i)
+                transposes(i, True)
+            if i + 2 < O:
+                quant_w(i + 2)
+            if 0 <= i - 1:
+                quant_tokens(i - 1, tcod[:, i - 1, :], tscl[:, i - 1, :])
+
+        def add_lin2(b, stage, tmps, g, ysl):
+            osl = slice(g * OGRP, (g + 1) * OGRP)
+            nc.vector.scalar_tensor_tensor(
+                out=stage[:, ysl, osl],
+                in0=lin2bs[b][:, ysl, osl],
+                scalar=bwn[:, 1:2],
+                in1=tmps[g][:, :, ysl].rearrange("p k y -> p y k"),
+                op0=ALU.mult,
+                op1=ALU.add,
+            )
+
+        for b in range(B):
+            cols = slice(b * L, (b + 1) * L)
+            stage = work.tile([P, L, O], F32, name="stage", tag="stage", bufs=2)
+            tmps = []
+            for g in range(O // OGRP):
+                pb = psum.tile([P, OGRP, L], F32, name="pair", tag="bank")
+                for k in range(OGRP):
+                    o = g * OGRP + k
+                    nc.tensor.matmul_mx(
+                        out=pb[:, k, :],
+                        lhsT=tcod[:, o, cols].bitcast(FP8X4),
+                        lhsT_scale=tscl[:, o, cols],
+                        rhs=x2c[:, cols].bitcast(FP8X4),
+                        rhs_scale=x2s[:, cols],
+                        start=True,
+                        stop=True,
+                    )
+                tmp = work.tile([P, OGRP, L], F32, name="tmp", tag="tmp", bufs=8)
+                for k in range(OGRP):
+                    o = g * OGRP + k
+                    xcol = xterm[:, b * O + o : b * O + o + 1]
+                    if o % V_READ_EVERY == V_READ_EVERY - 1:
+                        nc.vector.tensor_scalar(out=tmp[:, k, :], in0=pb[:, k, :], scalar1=bwn[:, 0:1], scalar2=xcol, op0=ALU.mult, op1=ALU.add)
+                    else:
+                        nc.scalar.activation(out=tmp[:, k, :], in_=pb[:, k, :], func=ACT.Identity, bias=xcol, scale=bwn[:, 0:1])
+                tmps.append(tmp)
+                if b < B - 1:
+                    add_lin2(b, stage, tmps, g, slice(0, L))
+            if b < B - 1:
+                nc.sync.dma_start(out=out[b], in_=stage[:])
+            else:
+                for y0 in range(0, L, YH):
+                    ysl = slice(y0, y0 + YH)
+                    for g in range(O // OGRP):
+                        add_lin2(b, stage, tmps, g, ysl)
+                    nc.sync.dma_start(out=out[b, :, ysl, :], in_=stage[:, ysl, :])

@@ -19,10 +19,9 @@ PACK = 4
 BANK_DT = BF16
 OGRP = 4
 YH = 64
-V_READ_EVERY = 64
 W_BUFS = 5
-MANUAL = False
-V_COPY_Q = [1]
+X2_STEP = 2
+V_COPY_Q = []
 
 
 def tile_biaffine_pa_kernel(tc, x1, x2, bw, W_bil, t_ones, lin1, lin2, b_lin, out):
@@ -31,8 +30,6 @@ def tile_biaffine_pa_kernel(tc, x1, x2, bw, W_bil, t_ones, lin1, lin2, b_lin, ou
         keep = ctx.enter_context(tc.tile_pool(name="keep", bufs=1))
         work = ctx.enter_context(tc.tile_pool(name="work", bufs=2))
         psum = ctx.enter_context(tc.psum_pool(name="psum", bufs=8))
-        if MANUAL:
-            ctx.enter_context(tc.manual_schedule())
 
         bw_sb = keep.tile([P, 2], BF16, name="bw_sb", tag="bw_sb")
         nc.scalar.dma_start(out=bw_sb[:], in_=bw.partition_broadcast(P))
@@ -42,6 +39,11 @@ def tile_biaffine_pa_kernel(tc, x1, x2, bw, W_bil, t_ones, lin1, lin2, b_lin, ou
         nc.scalar.dma_start(out=t1_sb[:], in_=t_ones.rearrange("b x o -> x b o"))
         l1_sb = keep.tile([P, B, O], BF16, name="l1_sb", tag="l1_sb")
         nc.scalar.dma_start(out=l1_sb[:], in_=lin1.rearrange("b x o -> x b o"))
+
+        warm = keep.tile([P, 1], F32, name="warm", tag="warm")
+        nc.vector.memset(warm[:], 0.0)
+        warm2 = keep.tile([P, 1], F32, name="warm2", tag="warm2")
+        nc.scalar.activation(out=warm2[:], in_=warm[:], func=ACT.Exp)
 
         ident = keep.tile([P, P], F32, name="ident", tag="ident")
         make_identity(nc, ident[:])
@@ -76,12 +78,19 @@ def tile_biaffine_pa_kernel(tc, x1, x2, bw, W_bil, t_ones, lin1, lin2, b_lin, ou
             nc.sync.dma_start(out=l2[:].rearrange("p y o -> p (y o)"), in_=lin2[b].rearrange("y o -> (y o)").partition_broadcast(P))
             lin2bs[b] = l2
 
-        def interleave_w(o, copies):
+        def interleave_w(o, second):
             g = work.tile([P, D, PACK], BF16, name="wgrp", tag="wgrp", bufs=3, align_bytes=64)
-            dst = g[:].rearrange("p (u c e) s -> p u c s e", u=2, e=2)
-            src = wraw[o][:].rearrange("p s (c u e) -> p u c s e", u=2, e=2)
-            for u in range(2):
-                copies[u](out=dst[:, u], in_=src[:, u])
+            raw = wraw[o]
+            nc.scalar.copy(
+                out=g[:].rearrange("p (u c e) s -> p u c s e", u=2, e=2)[:, 0],
+                in_=raw[:].rearrange("p s (c u e) -> p u c s e", u=2, e=2)[:, 0],
+            )
+            dst = g[:].rearrange("p (u c e) s -> p u c e s", u=2, e=2)[:, 1]
+            src = raw[:].rearrange("p s (c u e) -> p u c e s", u=2, e=2)[:, 1]
+            if second == "vector":
+                nc.vector.tensor_copy(out=dst, in_=src)
+            else:
+                nc.gpsimd.tensor_scalar(out=dst, in0=src, scalar1=1.0, scalar2=0.0, op0=ALU.mult, op1=ALU.add)
             wgrp[o] = g
 
         def quant_w(o):
@@ -162,13 +171,18 @@ def tile_biaffine_pa_kernel(tc, x1, x2, bw, W_bil, t_ones, lin1, lin2, b_lin, ou
         nc.vector.tensor_scalar(out=nmax[:], in0=bmax[:], scalar1=-1.0, scalar2=None, op0=ALU.mult)
         bexp = keep.tile([P, 2], F32, name="bexp", tag="bexp")
         nc.scalar.activation(out=bexp[:], in_=bwf[:], func=ACT.Exp, bias=nmax[:], scale=1.0)
+
+        transposes("x1", False)
+        copy_out("x1", [1])
+        interleave_w(0, "vector")
+        quant_tokens("x1", x1c[:], x1s[:])
+
         bsum = keep.tile([P, 1], F32, name="bsum", tag="bsum")
         nc.vector.tensor_tensor(out=bsum[:], in0=bexp[:, 0:1], in1=bexp[:, 1:2], op=ALU.add)
         brec = keep.tile([P, 1], F32, name="brec", tag="brec")
         nc.vector.reciprocal(out=brec[:], in_=bsum[:])
         bwn = keep.tile([P, 2], F32, name="bwn", tag="bwn")
         nc.vector.tensor_scalar(out=bwn[:], in0=bexp[:], scalar1=brec[:], scalar2=None, op0=ALU.mult)
-
         lsum = keep.tile([P, B, O], F32, name="lsum", tag="lsum")
         nc.vector.tensor_tensor(out=lsum[:], in0=l1_sb[:], in1=bl_sb[:].unsqueeze(1).to_broadcast([P, B, O]), op=ALU.add)
         lscl = keep.tile([P, B * O], F32, name="lscl", tag="lscl")
@@ -176,21 +190,14 @@ def tile_biaffine_pa_kernel(tc, x1, x2, bw, W_bil, t_ones, lin1, lin2, b_lin, ou
         xterm = keep.tile([P, B * O], F32, name="xterm", tag="xterm")
         nc.vector.scalar_tensor_tensor(out=xterm[:], in0=t1_sb[:].rearrange("p b o -> p (b o)"), scalar=bwn[:, 0:1], in1=lscl[:], op0=ALU.mult, op1=ALU.add)
 
-        transposes("x1", False)
-        copy_out("x1", [1])
-        interleave_w(0, [nc.scalar.copy, nc.vector.tensor_copy])
-        quant_tokens("x1", x1c[:], x1s[:])
-        transposes("x2", False)
-        copy_out("x2", [0, 1])
         quant_w(0)
-        interleave_w(1, [nc.scalar.copy, nc.scalar.copy])
-        quant_tokens("x2", x2c[:], x2s[:])
         stage1(0)
-        interleave_w(2, [nc.scalar.copy, nc.scalar.copy])
+        interleave_w(1, "gpsimd")
+        interleave_w(2, "gpsimd")
         quant_w(1)
 
-        for i in range(O + 1):
-            if 4 <= i + 4 < O:
+        def step(i):
+            if i + 4 < O:
                 load_w(i + 4)
             if (i + 2) % OGRP == 0 and (i + 2) // OGRP < O // OGRP:
                 load_bias((i + 2) // OGRP)
@@ -199,16 +206,26 @@ def tile_biaffine_pa_kernel(tc, x1, x2, bw, W_bil, t_ones, lin1, lin2, b_lin, ou
             if 0 <= i - 1:
                 copy_out(i - 1, V_COPY_Q)
             if i + 3 < O:
-                interleave_w(i + 3, [nc.scalar.copy, nc.scalar.copy])
+                interleave_w(i + 3, "gpsimd")
             if i + 1 < O:
                 stage1(i + 1)
             if i < O:
                 add_bias(i)
                 transposes(i, True)
-            if i + 2 < O:
-                quant_w(i + 2)
             if 0 <= i - 1:
                 quant_tokens(i - 1, tcod[:, i - 1, :], tscl[:, i - 1, :])
+            if i + 2 < O:
+                quant_w(i + 2)
+            if i == X2_STEP:
+                transposes("x2", False)
+                copy_out("x2", [])
+            if i == X2_STEP + 1:
+                quant_tokens("x2", x2c[:], x2s[:])
+
+        with tc.manual_schedule(engines={mybir.EngineType.DVE}):
+            for i in range(O):
+                step(i)
+        step(O)
 
         def add_lin2(b, stage, tmps, g, ysl):
             osl = slice(g * OGRP, (g + 1) * OGRP)
@@ -241,11 +258,7 @@ def tile_biaffine_pa_kernel(tc, x1, x2, bw, W_bil, t_ones, lin1, lin2, b_lin, ou
                 tmp = work.tile([P, OGRP, L], F32, name="tmp", tag="tmp", bufs=8)
                 for k in range(OGRP):
                     o = g * OGRP + k
-                    xcol = xterm[:, b * O + o : b * O + o + 1]
-                    if o % V_READ_EVERY == V_READ_EVERY - 1:
-                        nc.vector.tensor_scalar(out=tmp[:, k, :], in0=pb[:, k, :], scalar1=bwn[:, 0:1], scalar2=xcol, op0=ALU.mult, op1=ALU.add)
-                    else:
-                        nc.scalar.activation(out=tmp[:, k, :], in_=pb[:, k, :], func=ACT.Identity, bias=xcol, scale=bwn[:, 0:1])
+                    nc.scalar.activation(out=tmp[:, k, :], in_=pb[:, k, :], func=ACT.Identity, bias=xterm[:, b * O + o : b * O + o + 1], scale=bwn[:, 0:1])
                 tmps.append(tmp)
                 if b < B - 1:
                     add_lin2(b, stage, tmps, g, slice(0, L))

@@ -20,8 +20,7 @@ BANK_DT = BF16
 OGRP = 4
 YH = 64
 W_BUFS = 5
-X2_STEP = 2
-V_COPY_Q = []
+V_COPY_EVERY = 2
 
 
 def tile_biaffine_pa_kernel(tc, x1, x2, bw, W_bil, t_ones, lin1, lin2, b_lin, out):
@@ -47,6 +46,8 @@ def tile_biaffine_pa_kernel(tc, x1, x2, bw, W_bil, t_ones, lin1, lin2, b_lin, ou
 
         ident = keep.tile([P, P], F32, name="ident", tag="ident")
         make_identity(nc, ident[:])
+        ident_bf = keep.tile([P, P], BF16, name="ident_bf", tag="ident_bf")
+        make_identity(nc, ident_bf[:])
 
         x1c = keep.tile([P, B * L], U32, name="x1c", tag="x1c", align_bytes=64)
         x1s = keep.tile([P, B * L], U8, name="x1s", tag="x1s", align_bytes=64)
@@ -78,19 +79,24 @@ def tile_biaffine_pa_kernel(tc, x1, x2, bw, W_bil, t_ones, lin1, lin2, b_lin, ou
             nc.sync.dma_start(out=l2[:].rearrange("p y o -> p (y o)"), in_=lin2[b].rearrange("y o -> (y o)").partition_broadcast(P))
             lin2bs[b] = l2
 
-        def interleave_w(o, second):
+        def interleave_w(o, by_pe):
             g = work.tile([P, D, PACK], BF16, name="wgrp", tag="wgrp", bufs=3, align_bytes=64)
             raw = wraw[o]
             nc.scalar.copy(
                 out=g[:].rearrange("p (u c e) s -> p u c s e", u=2, e=2)[:, 0],
                 in_=raw[:].rearrange("p s (c u e) -> p u c s e", u=2, e=2)[:, 0],
             )
-            dst = g[:].rearrange("p (u c e) s -> p u c e s", u=2, e=2)[:, 1]
             src = raw[:].rearrange("p s (c u e) -> p u c e s", u=2, e=2)[:, 1]
-            if second == "vector":
-                nc.vector.tensor_copy(out=dst, in_=src)
+            if by_pe:
+                pw = psum.tile([P, 2, P // 2, 2, PACK], BF16, name="pw", tag="bank")
+                for h in range(2):
+                    nc.tensor.matmul(out=pw[:, h], lhsT=ident_bf[:], rhs=src[:, h * (P // 2) : (h + 1) * (P // 2)], start=True, stop=True)
+                nc.scalar.copy(
+                    out=g[:].rearrange("p (u n) s -> p u (n s)", u=2)[:, 1],
+                    in_=pw[:].rearrange("p h c e s -> p (h c e s)"),
+                )
             else:
-                nc.gpsimd.tensor_scalar(out=dst, in0=src, scalar1=1.0, scalar2=0.0, op0=ALU.mult, op1=ALU.add)
+                nc.vector.tensor_copy(out=g[:].rearrange("p (u c e) s -> p u c e s", u=2, e=2)[:, 1], in_=src)
             wgrp[o] = g
 
         def quant_w(o):
@@ -171,18 +177,13 @@ def tile_biaffine_pa_kernel(tc, x1, x2, bw, W_bil, t_ones, lin1, lin2, b_lin, ou
         nc.vector.tensor_scalar(out=nmax[:], in0=bmax[:], scalar1=-1.0, scalar2=None, op0=ALU.mult)
         bexp = keep.tile([P, 2], F32, name="bexp", tag="bexp")
         nc.scalar.activation(out=bexp[:], in_=bwf[:], func=ACT.Exp, bias=nmax[:], scale=1.0)
-
-        transposes("x1", False)
-        copy_out("x1", [1])
-        interleave_w(0, "vector")
-        quant_tokens("x1", x1c[:], x1s[:])
-
         bsum = keep.tile([P, 1], F32, name="bsum", tag="bsum")
         nc.vector.tensor_tensor(out=bsum[:], in0=bexp[:, 0:1], in1=bexp[:, 1:2], op=ALU.add)
         brec = keep.tile([P, 1], F32, name="brec", tag="brec")
         nc.vector.reciprocal(out=brec[:], in_=bsum[:])
         bwn = keep.tile([P, 2], F32, name="bwn", tag="bwn")
         nc.vector.tensor_scalar(out=bwn[:], in0=bexp[:], scalar1=brec[:], scalar2=None, op0=ALU.mult)
+
         lsum = keep.tile([P, B, O], F32, name="lsum", tag="lsum")
         nc.vector.tensor_tensor(out=lsum[:], in0=l1_sb[:], in1=bl_sb[:].unsqueeze(1).to_broadcast([P, B, O]), op=ALU.add)
         lscl = keep.tile([P, B * O], F32, name="lscl", tag="lscl")
@@ -190,42 +191,39 @@ def tile_biaffine_pa_kernel(tc, x1, x2, bw, W_bil, t_ones, lin1, lin2, b_lin, ou
         xterm = keep.tile([P, B * O], F32, name="xterm", tag="xterm")
         nc.vector.scalar_tensor_tensor(out=xterm[:], in0=t1_sb[:].rearrange("p b o -> p (b o)"), scalar=bwn[:, 0:1], in1=lscl[:], op0=ALU.mult, op1=ALU.add)
 
+        transposes("x1", False)
+        copy_out("x1", [1])
+        interleave_w(0, False)
+        quant_tokens("x1", x1c[:], x1s[:])
+        transposes("x2", False)
+        copy_out("x2", [0, 1])
         quant_w(0)
+        interleave_w(1, True)
+        quant_tokens("x2", x2c[:], x2s[:])
         stage1(0)
-        interleave_w(1, "gpsimd")
-        interleave_w(2, "gpsimd")
+        interleave_w(2, True)
         quant_w(1)
 
-        def step(i):
-            if i + 4 < O:
+        for i in range(O + 1):
+            if 4 <= i + 4 < O:
                 load_w(i + 4)
             if (i + 2) % OGRP == 0 and (i + 2) // OGRP < O // OGRP:
                 load_bias((i + 2) // OGRP)
             if O - 16 <= i < O and i % 4 == 0:
                 load_lin2((i - (O - 16)) // 4)
             if 0 <= i - 1:
-                copy_out(i - 1, V_COPY_Q)
+                copy_out(i - 1, [1] if V_COPY_EVERY and (i - 1) % V_COPY_EVERY == V_COPY_EVERY - 1 else [])
             if i + 3 < O:
-                interleave_w(i + 3, "gpsimd")
+                interleave_w(i + 3, True)
             if i + 1 < O:
                 stage1(i + 1)
             if i < O:
                 add_bias(i)
                 transposes(i, True)
-            if 0 <= i - 1:
-                quant_tokens(i - 1, tcod[:, i - 1, :], tscl[:, i - 1, :])
             if i + 2 < O:
                 quant_w(i + 2)
-            if i == X2_STEP:
-                transposes("x2", False)
-                copy_out("x2", [])
-            if i == X2_STEP + 1:
-                quant_tokens("x2", x2c[:], x2s[:])
-
-        with tc.manual_schedule(engines={mybir.EngineType.DVE}):
-            for i in range(O):
-                step(i)
-        step(O)
+            if 0 <= i - 1:
+                quant_tokens(i - 1, tcod[:, i - 1, :], tscl[:, i - 1, :])
 
         def add_lin2(b, stage, tmps, g, ysl):
             osl = slice(g * OGRP, (g + 1) * OGRP)
@@ -258,7 +256,8 @@ def tile_biaffine_pa_kernel(tc, x1, x2, bw, W_bil, t_ones, lin1, lin2, b_lin, ou
                 tmp = work.tile([P, OGRP, L], F32, name="tmp", tag="tmp", bufs=8)
                 for k in range(OGRP):
                     o = g * OGRP + k
-                    nc.scalar.activation(out=tmp[:, k, :], in_=pb[:, k, :], func=ACT.Identity, bias=xterm[:, b * O + o : b * O + o + 1], scale=bwn[:, 0:1])
+                    xcol = xterm[:, b * O + o : b * O + o + 1]
+                    nc.scalar.activation(out=tmp[:, k, :], in_=pb[:, k, :], func=ACT.Identity, bias=xcol, scale=bwn[:, 0:1])
                 tmps.append(tmp)
                 if b < B - 1:
                     add_lin2(b, stage, tmps, g, slice(0, L))

@@ -19,8 +19,10 @@ PACK = 4
 BANK_DT = BF16
 OGRP = 4
 YH = 64
+V_READ_EVERY = 64
 W_BUFS = 5
-V_COPY_EVERY = 2
+C_SPLIT = 78
+V_COPY_Q = []
 
 
 def tile_biaffine_pa_kernel(tc, x1, x2, bw, W_bil, t_ones, lin1, lin2, b_lin, out):
@@ -46,8 +48,6 @@ def tile_biaffine_pa_kernel(tc, x1, x2, bw, W_bil, t_ones, lin1, lin2, b_lin, ou
 
         ident = keep.tile([P, P], F32, name="ident", tag="ident")
         make_identity(nc, ident[:])
-        ident_bf = keep.tile([P, P], BF16, name="ident_bf", tag="ident_bf")
-        make_identity(nc, ident_bf[:])
 
         x1c = keep.tile([P, B * L], U32, name="x1c", tag="x1c", align_bytes=64)
         x1s = keep.tile([P, B * L], U8, name="x1s", tag="x1s", align_bytes=64)
@@ -79,24 +79,14 @@ def tile_biaffine_pa_kernel(tc, x1, x2, bw, W_bil, t_ones, lin1, lin2, b_lin, ou
             nc.sync.dma_start(out=l2[:].rearrange("p y o -> p (y o)"), in_=lin2[b].rearrange("y o -> (y o)").partition_broadcast(P))
             lin2bs[b] = l2
 
-        def interleave_w(o, by_pe):
+        def interleave_w(o, c_split):
             g = work.tile([P, D, PACK], BF16, name="wgrp", tag="wgrp", bufs=3, align_bytes=64)
-            raw = wraw[o]
-            nc.scalar.copy(
-                out=g[:].rearrange("p (u c e) s -> p u c s e", u=2, e=2)[:, 0],
-                in_=raw[:].rearrange("p s (c u e) -> p u c s e", u=2, e=2)[:, 0],
-            )
-            src = raw[:].rearrange("p s (c u e) -> p u c e s", u=2, e=2)[:, 1]
-            if by_pe:
-                pw = psum.tile([P, 2, P // 2, 2, PACK], BF16, name="pw", tag="bank")
-                for h in range(2):
-                    nc.tensor.matmul(out=pw[:, h], lhsT=ident_bf[:], rhs=src[:, h * (P // 2) : (h + 1) * (P // 2)], start=True, stop=True)
-                nc.scalar.copy(
-                    out=g[:].rearrange("p (u n) s -> p u (n s)", u=2)[:, 1],
-                    in_=pw[:].rearrange("p h c e s -> p (h c e s)"),
-                )
-            else:
-                nc.vector.tensor_copy(out=g[:].rearrange("p (u c e) s -> p u c e s", u=2, e=2)[:, 1], in_=src)
+            dst = g[:].rearrange("p (u c e) s -> p c u e s", u=2, e=2)
+            src = wraw[o][:].rearrange("p s (c u e) -> p c u e s", u=2, e=2)
+            half = c_split // 2
+            nc.scalar.copy(out=dst[:, 0:half], in_=src[:, 0:half])
+            nc.scalar.copy(out=dst[:, half:c_split], in_=src[:, half:c_split])
+            nc.vector.tensor_copy(out=dst[:, c_split:], in_=src[:, c_split:])
             wgrp[o] = g
 
         def quant_w(o):
@@ -193,15 +183,15 @@ def tile_biaffine_pa_kernel(tc, x1, x2, bw, W_bil, t_ones, lin1, lin2, b_lin, ou
 
         transposes("x1", False)
         copy_out("x1", [1])
-        interleave_w(0, False)
+        interleave_w(0, P // 2)
         quant_tokens("x1", x1c[:], x1s[:])
         transposes("x2", False)
         copy_out("x2", [0, 1])
         quant_w(0)
-        interleave_w(1, True)
+        interleave_w(1, C_SPLIT)
         quant_tokens("x2", x2c[:], x2s[:])
         stage1(0)
-        interleave_w(2, True)
+        interleave_w(2, C_SPLIT)
         quant_w(1)
 
         for i in range(O + 1):
@@ -212,9 +202,9 @@ def tile_biaffine_pa_kernel(tc, x1, x2, bw, W_bil, t_ones, lin1, lin2, b_lin, ou
             if O - 16 <= i < O and i % 4 == 0:
                 load_lin2((i - (O - 16)) // 4)
             if 0 <= i - 1:
-                copy_out(i - 1, [1] if V_COPY_EVERY and (i - 1) % V_COPY_EVERY == V_COPY_EVERY - 1 else [])
+                copy_out(i - 1, V_COPY_Q)
             if i + 3 < O:
-                interleave_w(i + 3, True)
+                interleave_w(i + 3, C_SPLIT)
             if i + 1 < O:
                 stage1(i + 1)
             if i < O:
@@ -257,7 +247,10 @@ def tile_biaffine_pa_kernel(tc, x1, x2, bw, W_bil, t_ones, lin1, lin2, b_lin, ou
                 for k in range(OGRP):
                     o = g * OGRP + k
                     xcol = xterm[:, b * O + o : b * O + o + 1]
-                    nc.scalar.activation(out=tmp[:, k, :], in_=pb[:, k, :], func=ACT.Identity, bias=xcol, scale=bwn[:, 0:1])
+                    if o % V_READ_EVERY == V_READ_EVERY - 1:
+                        nc.vector.tensor_scalar(out=tmp[:, k, :], in0=pb[:, k, :], scalar1=bwn[:, 0:1], scalar2=xcol, op0=ALU.mult, op1=ALU.add)
+                    else:
+                        nc.scalar.activation(out=tmp[:, k, :], in_=pb[:, k, :], func=ACT.Identity, bias=xcol, scale=bwn[:, 0:1])
                 tmps.append(tmp)
                 if b < B - 1:
                     add_lin2(b, stage, tmps, g, slice(0, L))

@@ -20,9 +20,10 @@ BANK_DT = BF16
 OGRP = 4
 YH = 64
 V_READ_EVERY = 64
-W_BUFS = 5
+W_BUFS = 6
 C_SPLIT = 78
-V_COPY_Q = []
+OP = 2
+NP = O // OP
 
 
 def tile_biaffine_pa_kernel(tc, x1, x2, bw, W_bil, t_ones, lin1, lin2, b_lin, out):
@@ -79,28 +80,29 @@ def tile_biaffine_pa_kernel(tc, x1, x2, bw, W_bil, t_ones, lin1, lin2, b_lin, ou
             nc.sync.dma_start(out=l2[:].rearrange("p y o -> p (y o)"), in_=lin2[b].rearrange("y o -> (y o)").partition_broadcast(P))
             lin2bs[b] = l2
 
-        def interleave_w(o, c_split):
-            g = work.tile([P, D, PACK], BF16, name="wgrp", tag="wgrp", bufs=3, align_bytes=64)
-            dst = g[:].rearrange("p (u c e) s -> p c u e s", u=2, e=2)
-            src = wraw[o][:].rearrange("p s (c u e) -> p c u e s", u=2, e=2)
+        def interleave_w(i, c_split):
+            g = work.tile([P, OP * D, PACK], BF16, name="wgrp", tag="wgrp", bufs=2, align_bytes=64)
             half = c_split // 2
-            nc.scalar.copy(out=dst[:, 0:half], in_=src[:, 0:half])
-            nc.scalar.copy(out=dst[:, half:c_split], in_=src[:, half:c_split])
-            nc.vector.tensor_copy(out=dst[:, c_split:], in_=src[:, c_split:])
-            wgrp[o] = g
+            for q in range(OP):
+                dst = g[:].rearrange("p (u q c e) s -> p q c u e s", u=2, q=OP, e=2)[:, q]
+                src = wraw[OP * i + q][:].rearrange("p s (c u e) -> p c u e s", u=2, e=2)
+                nc.scalar.copy(out=dst[:, 0:half], in_=src[:, 0:half])
+                nc.scalar.copy(out=dst[:, half:c_split], in_=src[:, half:c_split])
+                nc.vector.tensor_copy(out=dst[:, c_split:], in_=src[:, c_split:])
+            wgrp[i] = g
 
-        def quant_w(o):
-            wc = work.tile([P, D], U32, name="wc", tag="wc", bufs=3, align_bytes=64)
-            ws = work.tile([P, D], U8, name="ws", tag="ws", bufs=3, align_bytes=64)
-            nc.vector.quantize_mx(out=wc[:].bitcast(FP8X4), scales=ws[:], in_=wgrp[o][:].rearrange("p j s -> p (j s)"))
-            wq[o] = (wc, ws)
+        def quant_w(i):
+            wc = work.tile([P, OP * D], U32, name="wc", tag="wc", bufs=2, align_bytes=64)
+            ws = work.tile([P, OP * D], U8, name="ws", tag="ws", bufs=2, align_bytes=64)
+            nc.vector.quantize_mx(out=wc[:].bitcast(FP8X4), scales=ws[:], in_=wgrp[i][:].rearrange("p j s -> p (j s)"))
+            wq[i] = (wc, ws)
 
         def stage1(o):
             wc, ws = wq[o]
             banks[o] = []
             for b in range(B):
                 cols = slice(b * L, (b + 1) * L)
-                bank = psum.tile([P, D], BANK_DT, name="bank", tag="bank")
+                bank = psum.tile([P, OP * D], BANK_DT, name="bank", tag="bank")
                 nc.tensor.matmul_mx(
                     out=bank[:],
                     lhsT=x1c[:, cols].bitcast(FP8X4),
@@ -112,35 +114,39 @@ def tile_biaffine_pa_kernel(tc, x1, x2, bw, W_bil, t_ones, lin1, lin2, b_lin, ou
                 )
                 banks[o].append(bank)
 
-        def add_bias(o):
-            tb = work.tile([P, B, D], BF16, name="tb", tag="tb", bufs=2, align_bytes=64)
+        def add_bias(i):
+            tb = work.tile([P, B, OP * D], BF16, name="tb", tag="tb", bufs=2, align_bytes=64)
+            per = OGRP // OP
+            rows = biases[i // per][:].rearrange("p g d -> p (g d)")[:, (i % per) * OP * D : (i % per + 1) * OP * D]
             for b in range(B):
                 nc.vector.tensor_tensor(
-                    out=tb[:, b, :].rearrange("p (u c e) -> p u c e", u=2, e=2),
-                    in0=banks[o][b][:].rearrange("p (u c e) -> p u c e", u=2, e=2),
-                    in1=biases[o // OGRP][:, o % OGRP, :].rearrange("p (c u e) -> p u c e", u=2, e=2),
+                    out=tb[:, b, :].rearrange("p (u x e) -> p u x e", u=2, e=2),
+                    in0=banks[i][b][:].rearrange("p (u x e) -> p u x e", u=2, e=2),
+                    in1=rows.rearrange("p (x u e) -> p u x e", u=2, e=2),
                     op=ALU.add,
                 )
-            tbs[o] = tb
+            tbs[i] = tb
 
-        def transposes(key, permuted):
+        def transposes(key, n_o):
             words = tbs[key][:].bitcast(F32)
             xts[key] = []
-            for q in range(2):
-                xt = psum.tile([P, 2, 2, L], F32, name="xt", tag="bank")
-                for h in range(2):
-                    for u in range(2):
-                        if permuted:
-                            sel = words[:, 2 * q + h, u * P : (u + 1) * P]
-                        else:
-                            sel = words[:, 2 * q + h, u : D // 2 : 2]
-                        nc.tensor.transpose(xt[:, h, u, :], sel, ident[:])
-                xts[key].append(xt)
+            for q in range(max(n_o, 1)):
+                for r in range(2):
+                    xt = psum.tile([P, 2, 2, L], F32, name="xt", tag="bank")
+                    for h in range(2):
+                        for u in range(2):
+                            if n_o:
+                                sel = words[:, 2 * r + h, (u * n_o + q) * P : (u * n_o + q + 1) * P]
+                            else:
+                                sel = words[:, 2 * r + h, u : D // 2 : 2]
+                            nc.tensor.transpose(xt[:, h, u, :], sel, ident[:])
+                    xts[key].append(xt)
 
         def copy_out(key, v_q):
-            tg = work.tile([P, B * L * PACK], BF16, name="tg", tag="tg", bufs=2, align_bytes=64)
-            gw = tg[:].bitcast(F32).rearrange("p (b x u) -> p b x u", b=B, u=2)
-            for q in range(2):
+            n = len(xts[key])
+            tg = work.tile([P, n // 2 * B * L * PACK], BF16, name="tg", tag="tg", bufs=2, align_bytes=64)
+            gw = tg[:].bitcast(F32).rearrange("p (b x u) -> p b x u", b=n * 2, u=2)
+            for q in range(n):
                 src = xts[key][q][:].rearrange("p h u x -> p h x u")
                 if q in v_q:
                     nc.vector.tensor_copy(out=gw[:, 2 * q : 2 * q + 2], in_=src)
@@ -181,39 +187,39 @@ def tile_biaffine_pa_kernel(tc, x1, x2, bw, W_bil, t_ones, lin1, lin2, b_lin, ou
         xterm = keep.tile([P, B * O], F32, name="xterm", tag="xterm")
         nc.vector.scalar_tensor_tensor(out=xterm[:], in0=t1_sb[:].rearrange("p b o -> p (b o)"), scalar=bwn[:, 0:1], in1=lscl[:], op0=ALU.mult, op1=ALU.add)
 
-        transposes("x1", False)
+        transposes("x1", 0)
         copy_out("x1", [1])
         interleave_w(0, P // 2)
         quant_tokens("x1", x1c[:], x1s[:])
-        transposes("x2", False)
+        transposes("x2", 0)
         copy_out("x2", [0, 1])
         quant_w(0)
-        interleave_w(1, C_SPLIT)
         quant_tokens("x2", x2c[:], x2s[:])
         stage1(0)
-        interleave_w(2, C_SPLIT)
-        quant_w(1)
+        interleave_w(1, C_SPLIT)
 
-        for i in range(O + 1):
-            if 4 <= i + 4 < O:
-                load_w(i + 4)
-            if (i + 2) % OGRP == 0 and (i + 2) // OGRP < O // OGRP:
-                load_bias((i + 2) // OGRP)
-            if O - 16 <= i < O and i % 4 == 0:
-                load_lin2((i - (O - 16)) // 4)
+        for i in range(NP + 1):
+            for o in (OP * (i + 2), OP * (i + 2) + 1):
+                if o < O:
+                    load_w(o)
+            if i % 2 == 0 and i // 2 + 1 < O // OGRP:
+                load_bias(i // 2 + 1)
+            if NP - 8 <= i < NP and i % 2 == 0:
+                load_lin2((i - (NP - 8)) // 2)
+            if i + 1 < NP:
+                quant_w(i + 1)
             if 0 <= i - 1:
-                copy_out(i - 1, V_COPY_Q)
-            if i + 3 < O:
-                interleave_w(i + 3, C_SPLIT)
-            if i + 1 < O:
+                copy_out(i - 1, [])
+            if i + 2 < NP:
+                interleave_w(i + 2, C_SPLIT)
+            if i + 1 < NP:
                 stage1(i + 1)
-            if i < O:
+            if i < NP:
                 add_bias(i)
-                transposes(i, True)
-            if i + 2 < O:
-                quant_w(i + 2)
+                transposes(i, OP)
             if 0 <= i - 1:
-                quant_tokens(i - 1, tcod[:, i - 1, :], tscl[:, i - 1, :])
+                osl = slice(OP * (i - 1), OP * i)
+                quant_tokens(i - 1, tcod[:, osl, :].rearrange("p o n -> p (o n)"), tscl[:, osl, :].rearrange("p o n -> p (o n)"))
 
         def add_lin2(b, stage, tmps, g, ysl):
             osl = slice(g * OGRP, (g + 1) * OGRP)
@@ -228,7 +234,7 @@ def tile_biaffine_pa_kernel(tc, x1, x2, bw, W_bil, t_ones, lin1, lin2, b_lin, ou
 
         for b in range(B):
             cols = slice(b * L, (b + 1) * L)
-            stage = work.tile([P, L, O], F32, name="stage", tag="stage", bufs=2)
+            stage = work.tile([P, L, O], F32, name="stage", tag="tb", bufs=2, align_bytes=64)
             tmps = []
             for g in range(O // OGRP):
                 pb = psum.tile([P, OGRP, L], F32, name="pair", tag="bank")
@@ -243,7 +249,9 @@ def tile_biaffine_pa_kernel(tc, x1, x2, bw, W_bil, t_ones, lin1, lin2, b_lin, ou
                         start=True,
                         stop=True,
                     )
-                tmp = work.tile([P, OGRP, L], F32, name="tmp", tag="tmp", bufs=8)
+                if g % 4 == 0:
+                    tmp4 = work.tile([P, 4, OGRP, L], F32, name="tmp4", tag="tg", bufs=2, align_bytes=64)
+                tmp = tmp4[:, g % 4]
                 for k in range(OGRP):
                     o = g * OGRP + k
                     xcol = xterm[:, b * O + o : b * O + o + 1]

@@ -21,7 +21,8 @@ OGRP = 4
 YH = 64
 V_READ_EVERY = 64
 W_BUFS = 6
-C_SPLIT = 78
+C_SPLIT = 64
+G_SPLIT = 84
 OP = 2
 NP = O // OP
 
@@ -80,15 +81,15 @@ def tile_biaffine_pa_kernel(tc, x1, x2, bw, W_bil, t_ones, lin1, lin2, b_lin, ou
             nc.sync.dma_start(out=l2[:].rearrange("p y o -> p (y o)"), in_=lin2[b].rearrange("y o -> (y o)").partition_broadcast(P))
             lin2bs[b] = l2
 
-        def interleave_w(i, c_split):
+        def interleave_w(i, c_split, g_split):
             g = work.tile([P, OP * D, PACK], BF16, name="wgrp", tag="wgrp", bufs=2, align_bytes=64)
-            half = c_split // 2
             for q in range(OP):
                 dst = g[:].rearrange("p (u q c e) s -> p q c u e s", u=2, q=OP, e=2)[:, q]
                 src = wraw[OP * i + q][:].rearrange("p s (c u e) -> p c u e s", u=2, e=2)
-                nc.scalar.copy(out=dst[:, 0:half], in_=src[:, 0:half])
-                nc.scalar.copy(out=dst[:, half:c_split], in_=src[:, half:c_split])
-                nc.vector.tensor_copy(out=dst[:, c_split:], in_=src[:, c_split:])
+                nc.scalar.copy(out=dst[:, 0:c_split], in_=src[:, 0:c_split])
+                nc.vector.tensor_copy(out=dst[:, c_split:g_split], in_=src[:, c_split:g_split])
+                if g_split < P:
+                    nc.gpsimd.tensor_scalar(out=dst[:, g_split:], in0=src[:, g_split:], scalar1=1.0, scalar2=0.0, op0=ALU.mult, op1=ALU.add)
             wgrp[i] = g
 
         def quant_w(i):
@@ -121,8 +122,8 @@ def tile_biaffine_pa_kernel(tc, x1, x2, bw, W_bil, t_ones, lin1, lin2, b_lin, ou
             for b in range(B):
                 nc.vector.tensor_tensor(
                     out=tb[:, b, :].rearrange("p (u x e) -> p u x e", u=2, e=2),
-                    in0=banks[i][b][:].rearrange("p (u x e) -> p u x e", u=2, e=2),
-                    in1=rows.rearrange("p (x u e) -> p u x e", u=2, e=2),
+                    in0=rows.rearrange("p (x u e) -> p u x e", u=2, e=2),
+                    in1=banks[i][b][:].rearrange("p (u x e) -> p u x e", u=2, e=2),
                     op=ALU.add,
                 )
             tbs[i] = tb
@@ -189,37 +190,37 @@ def tile_biaffine_pa_kernel(tc, x1, x2, bw, W_bil, t_ones, lin1, lin2, b_lin, ou
 
         transposes("x1", 0)
         copy_out("x1", [1])
-        interleave_w(0, P // 2)
+        interleave_w(0, P // 2, P)
         quant_tokens("x1", x1c[:], x1s[:])
         transposes("x2", 0)
         copy_out("x2", [0, 1])
         quant_w(0)
         quant_tokens("x2", x2c[:], x2s[:])
         stage1(0)
-        interleave_w(1, C_SPLIT)
+        interleave_w(1, C_SPLIT, G_SPLIT)
 
-        for i in range(NP + 1):
-            for o in (OP * (i + 2), OP * (i + 2) + 1):
-                if o < O:
-                    load_w(o)
-            if i % 2 == 0 and i // 2 + 1 < O // OGRP:
-                load_bias(i // 2 + 1)
-            if NP - 8 <= i < NP and i % 2 == 0:
-                load_lin2((i - (NP - 8)) // 2)
-            if i + 1 < NP:
-                quant_w(i + 1)
-            if 0 <= i - 1:
-                copy_out(i - 1, [])
-            if i + 2 < NP:
-                interleave_w(i + 2, C_SPLIT)
-            if i + 1 < NP:
-                stage1(i + 1)
-            if i < NP:
-                add_bias(i)
-                transposes(i, OP)
-            if 0 <= i - 1:
-                osl = slice(OP * (i - 1), OP * i)
-                quant_tokens(i - 1, tcod[:, osl, :].rearrange("p o n -> p (o n)"), tscl[:, osl, :].rearrange("p o n -> p (o n)"))
+        with tc.manual_schedule(engines={mybir.EngineType.DVE}):
+            for i in range(NP + 2):
+                for o in (OP * (i + 2), OP * (i + 2) + 1):
+                    if o < O:
+                        load_w(o)
+                if i % 2 == 0 and i // 2 + 1 < O // OGRP:
+                    load_bias(i // 2 + 1)
+                if NP - 8 <= i < NP and i % 2 == 0:
+                    load_lin2((i - (NP - 8)) // 2)
+                if 0 <= i - 1 < NP:
+                    copy_out(i - 1, [])
+                if 0 <= i - 2:
+                    osl = slice(OP * (i - 2), OP * (i - 1))
+                    quant_tokens(i - 2, tcod[:, osl, :].rearrange("p o n -> p (o n)"), tscl[:, osl, :].rearrange("p o n -> p (o n)"))
+                if i + 1 < NP:
+                    quant_w(i + 1)
+                    stage1(i + 1)
+                if i < NP:
+                    add_bias(i)
+                    transposes(i, OP)
+                if i + 2 < NP:
+                    interleave_w(i + 2, C_SPLIT, G_SPLIT)
 
         def add_lin2(b, stage, tmps, g, ysl):
             osl = slice(g * OGRP, (g + 1) * OGRP)

@@ -21,7 +21,7 @@ OGRP = 4
 YH = 64
 V_READ_EVERY = 64
 W_BUFS = 6
-C_SPLIT = 64
+C_SPLIT = 76
 G_SPLIT = 84
 OP = 2
 NP = O // OP
@@ -193,11 +193,10 @@ def tile_biaffine_pa_kernel(tc, x1, x2, bw, W_bil, t_ones, lin1, lin2, b_lin, ou
         interleave_w(0, P // 2, P)
         quant_tokens("x1", x1c[:], x1s[:])
         transposes("x2", 0)
-        copy_out("x2", [0, 1])
         quant_w(0)
-        quant_tokens("x2", x2c[:], x2s[:])
         stage1(0)
         interleave_w(1, C_SPLIT, G_SPLIT)
+        copy_out("x2", [])
 
         with tc.manual_schedule(engines={mybir.EngineType.DVE}):
             for i in range(NP + 2):
@@ -208,6 +207,8 @@ def tile_biaffine_pa_kernel(tc, x1, x2, bw, W_bil, t_ones, lin1, lin2, b_lin, ou
                     load_bias(i // 2 + 1)
                 if NP - 8 <= i < NP and i % 2 == 0:
                     load_lin2((i - (NP - 8)) // 2)
+                if i == 1:
+                    quant_tokens("x2", x2c[:], x2s[:])
                 if 0 <= i - 1 < NP:
                     copy_out(i - 1, [])
                 if 0 <= i - 2:

@@ -84,8 +84,8 @@ def tile_biaffine_pa_kernel(tc, x1, x2, bw, W_bil, t_ones, lin1, lin2, b_lin, ou
         def interleave_w(i, c_split, g_split):
             g = work.tile([P, OP * D, PACK], BF16, name="wgrp", tag="wgrp", bufs=2, align_bytes=64)
             for q in range(OP):
-                dst = g[:].rearrange("p (u q c e) s -> p q c u e s", u=2, q=OP, e=2)[:, q]
-                src = wraw[OP * i + q][:].rearrange("p s (c u e) -> p c u e s", u=2, e=2)
+                dst = g[:].rearrange("p (q c t) s -> p q c s t", q=OP, t=4)[:, q]
+                src = wraw[OP * i + q][:].rearrange("p s (c t) -> p c s t", t=4)
                 nc.scalar.copy(out=dst[:, 0:c_split], in_=src[:, 0:c_split])
                 nc.vector.tensor_copy(out=dst[:, c_split:g_split], in_=src[:, c_split:g_split])
                 if g_split < P:
@@ -121,9 +121,9 @@ def tile_biaffine_pa_kernel(tc, x1, x2, bw, W_bil, t_ones, lin1, lin2, b_lin, ou
             rows = biases[i // per][:].rearrange("p g d -> p (g d)")[:, (i % per) * OP * D : (i % per + 1) * OP * D]
             for b in range(B):
                 nc.vector.tensor_tensor(
-                    out=tb[:, b, :].rearrange("p (u x e) -> p u x e", u=2, e=2),
-                    in0=rows.rearrange("p (x u e) -> p u x e", u=2, e=2),
-                    in1=banks[i][b][:].rearrange("p (u x e) -> p u x e", u=2, e=2),
+                    out=tb[:, b, :],
+                    in0=rows,
+                    in1=banks[i][b][:],
                     op=ALU.add,
                 )
             tbs[i] = tb
@@ -137,7 +137,7 @@ def tile_biaffine_pa_kernel(tc, x1, x2, bw, W_bil, t_ones, lin1, lin2, b_lin, ou
                     for h in range(2):
                         for u in range(2):
                             if n_o:
-                                sel = words[:, 2 * r + h, (u * n_o + q) * P : (u * n_o + q + 1) * P]
+                                sel = words[:, 2 * r + h, q * D // 2 + u : (q + 1) * D // 2 : 2]
                             else:
                                 sel = words[:, 2 * r + h, u : D // 2 : 2]
                             nc.tensor.transpose(xt[:, h, u, :], sel, ident[:])

@@ -21,7 +21,7 @@ OGRP = 4
 YH = 64
 V_READ_EVERY = 64
 W_BUFS = 6
-C_SPLIT = 76
+C_SPLIT = 84
 G_SPLIT = 84
 OP = 2
 NP = O // OP
@@ -87,7 +87,8 @@ def tile_biaffine_pa_kernel(tc, x1, x2, bw, W_bil, t_ones, lin1, lin2, b_lin, ou
                 dst = g[:].rearrange("p (q c t) s -> p q c s t", q=OP, t=4)[:, q]
                 src = wraw[OP * i + q][:].rearrange("p s (c t) -> p c s t", t=4)
                 nc.scalar.copy(out=dst[:, 0:c_split], in_=src[:, 0:c_split])
-                nc.vector.tensor_copy(out=dst[:, c_split:g_split], in_=src[:, c_split:g_split])
+                if c_split < g_split:
+                    nc.vector.tensor_copy(out=dst[:, c_split:g_split], in_=src[:, c_split:g_split])
                 if g_split < P:
                     nc.gpsimd.tensor_scalar(out=dst[:, g_split:], in0=src[:, g_split:], scalar1=1.0, scalar2=0.0, op0=ALU.mult, op1=ALU.add)
             wgrp[i] = g

@@ -19,6 +19,7 @@ PACK = 4
 BANK_DT = BF16
 OGRP = 4
 YH = 64
+RUN = 16
 V_READ_EVERY = 64
 W_BUFS = 6
 C_SPLIT = 84
@@ -122,9 +123,9 @@ def tile_biaffine_pa_kernel(tc, x1, x2, bw, W_bil, t_ones, lin1, lin2, b_lin, ou
             rows = biases[i // per][:].rearrange("p g d -> p (g d)")[:, (i % per) * OP * D : (i % per + 1) * OP * D]
             for b in range(B):
                 nc.vector.tensor_tensor(
-                    out=tb[:, b, :],
-                    in0=rows,
-                    in1=banks[i][b][:],
+                    out=tb[:, b, :].rearrange("p (u a r) -> p a u r", u=2, r=RUN),
+                    in0=rows.rearrange("p (a u r) -> p a u r", u=2, r=RUN),
+                    in1=banks[i][b][:].rearrange("p (a u r) -> p a u r", u=2, r=RUN),
                     op=ALU.add,
                 )
             tbs[i] = tb
@@ -137,10 +138,12 @@ def tile_biaffine_pa_kernel(tc, x1, x2, bw, W_bil, t_ones, lin1, lin2, b_lin, ou
                     xt = psum.tile([P, 2, 2, L], F32, name="xt", tag="bank")
                     for h in range(2):
                         for u in range(2):
-                            if n_o:
-                                sel = words[:, 2 * r + h, q * D // 2 + u : (q + 1) * D // 2 : 2]
-                            else:
+                            if key == "x1":
                                 sel = words[:, 2 * r + h, u : D // 2 : 2]
+                            elif key == "x2":
+                                sel = words[:, u, (2 * r + h) * P : (2 * r + h + 1) * P]
+                            else:
+                                sel = words[:, 2 * r + h, (u * OP + q) * P : (u * OP + q + 1) * P]
                             nc.tensor.transpose(xt[:, h, u, :], sel, ident[:])
                     xts[key].append(xt)
 
@@ -158,6 +161,14 @@ def tile_biaffine_pa_kernel(tc, x1, x2, bw, W_bil, t_ones, lin1, lin2, b_lin, ou
 
         def quant_tokens(key, codes, scales):
             nc.vector.quantize_mx(out=codes.bitcast(FP8X4), scales=scales, in_=tgs[key][:])
+
+        def permute_x2():
+            x2p = keep.tile([P, 2, B * D // 2], BF16, name="x2p", tag="x2p", align_bytes=64)
+            nc.vector.tensor_copy(
+                out=x2p[:].rearrange("p u (n r) -> p n u r", r=RUN),
+                in_=tbs["x2"][:].rearrange("p b (a u r) -> p (b a) u r", u=2, r=RUN),
+            )
+            tbs["x2"] = x2p
 
         load_tokens(x1, "x1")
         load_w(0)
@@ -193,6 +204,7 @@ def tile_biaffine_pa_kernel(tc, x1, x2, bw, W_bil, t_ones, lin1, lin2, b_lin, ou
         copy_out("x1", [1])
         interleave_w(0, P // 2, P)
         quant_tokens("x1", x1c[:], x1s[:])
+        permute_x2()
         transposes("x2", 0)
         quant_w(0)
         stage1(0)

@@ -20,7 +20,10 @@ BANK_DT = BF16
 OGRP = 4
 YH = 64
 RUN = 16
-V_READ_EVERY = 64
+TERMS = 3
+E_STEP = 3
+LROW = TERMS * O
+HALF = O // OGRP // 2
 W_BUFS = 6
 C_SPLIT = 84
 G_SPLIT = 84
@@ -59,7 +62,7 @@ def tile_biaffine_pa_kernel(tc, x1, x2, bw, W_bil, t_ones, lin1, lin2, b_lin, ou
         tcod = keep.tile([P, O, B * L], U32, name="tcod", tag="tcod", align_bytes=64)
         tscl = keep.tile([P, O, B * L], U8, name="tscl", tag="tscl", align_bytes=64)
 
-        wraw, wgrp, wq, banks, tbs, xts, tgs, biases, lin2bs = {}, {}, {}, {}, {}, {}, {}, {}, {}
+        wraw, wgrp, wq, banks, tbs, xts, tgs, biases, exs = {}, {}, {}, {}, {}, {}, {}, {}, {}
 
         def load_tokens(x, key):
             raw = work.tile([P, B, D], BF16, name="xraw", tag="wraw", bufs=W_BUFS, align_bytes=64)
@@ -76,11 +79,6 @@ def tile_biaffine_pa_kernel(tc, x1, x2, bw, W_bil, t_ones, lin1, lin2, b_lin, ou
             bt = work.tile([P, OGRP, D], BF16, name="bias", tag="bias", bufs=2)
             nc.sync.dma_start(out=bt[:], in_=W_bil[c * OGRP : (c + 1) * OGRP, D, :].partition_broadcast(P))
             biases[c] = bt
-
-        def load_lin2(b):
-            l2 = work.tile([P, L, O], BF16, name="lin2b", tag="lin2b", bufs=4)
-            nc.sync.dma_start(out=l2[:].rearrange("p y o -> p (y o)"), in_=lin2[b].rearrange("y o -> (y o)").partition_broadcast(P))
-            lin2bs[b] = l2
 
         def interleave_w(i, c_split, g_split):
             g = work.tile([P, OP * D, PACK], BF16, name="wgrp", tag="wgrp", bufs=2, align_bytes=64)
@@ -200,6 +198,13 @@ def tile_biaffine_pa_kernel(tc, x1, x2, bw, W_bil, t_ones, lin1, lin2, b_lin, ou
         xterm = keep.tile([P, B * O], F32, name="xterm", tag="xterm")
         nc.vector.scalar_tensor_tensor(out=xterm[:], in0=t1_sb[:].rearrange("p b o -> p (b o)"), scalar=bwn[:, 0:1], in1=lscl[:], op0=ALU.mult, op1=ALU.add)
 
+        fold = keep.tile([P, O], F32, name="fold", tag="fold")
+        nc.gpsimd.tensor_tensor(out=fold[:], in0=ident[:, 0:O], in1=ident[:, O : 2 * O], op=ALU.add)
+        fold3 = keep.tile([P, O], F32, name="fold3", tag="fold3")
+        nc.gpsimd.tensor_tensor(out=fold3[:], in0=fold[:], in1=ident[:, 2 * O : 3 * O], op=ALU.add)
+        erhs = keep.tile([P, L, O], BF16, name="erhs", tag="erhs", align_bytes=64)
+        nc.gpsimd.tensor_scalar(out=erhs[:], in0=fold3[:].unsqueeze(1).to_broadcast([P, L, O]), scalar1=1.0, scalar2=0.0, op0=ALU.mult, op1=ALU.add)
+
         transposes("x1", 0)
         copy_out("x1", [1])
         interleave_w(0, P // 2, P)
@@ -211,6 +216,77 @@ def tile_biaffine_pa_kernel(tc, x1, x2, bw, W_bil, t_ones, lin1, lin2, b_lin, ou
         interleave_w(1, C_SPLIT, G_SPLIT)
         copy_out("x2", [])
 
+        ecoef = keep.tile([P, B, P], BF16, name="ecoef", tag="ecoef", align_bytes=64)
+        nc.vector.memset(ecoef[:], 0.0)
+        xrest = xterm
+        wrest = bwn[:, 1:2]
+        for t in range(TERMS):
+            xt_out = ecoef[:, :, t * O : (t + 1) * O]
+            wt_out = ecoef[:].rearrange("p b k -> p (b k)")[:, LROW + t : LROW + t + (B - 1) * (P + TERMS) + 1 : P + TERMS]
+            nc.vector.tensor_copy(out=xt_out, in_=xrest[:].rearrange("p (b o) -> p b o", b=B))
+            nc.vector.tensor_copy(out=wt_out, in_=wrest.to_broadcast([P, B]))
+            if t + 1 < TERMS:
+                xnext = keep.tile([P, B * O], F32, name="xrest%d" % t, tag="xrest%d" % t)
+                nc.vector.tensor_tensor(out=xnext[:].rearrange("p (b o) -> p b o", b=B), in0=xrest[:].rearrange("p (b o) -> p b o", b=B), in1=xt_out, op=ALU.subtract)
+                wnext = keep.tile([P, 1], F32, name="wrest%d" % t, tag="wrest%d" % t)
+                nc.vector.tensor_tensor(out=wnext[:], in0=wrest, in1=ecoef[:, 0, LROW + t : LROW + t + 1], op=ALU.subtract)
+                xrest = xnext
+                wrest = wnext[:]
+        identb = keep.tile([P, P], BF16, name="identb", tag="identb")
+        nc.vector.tensor_copy(out=identb[:], in_=ident[:])
+        elhs = keep.tile([P, B, P], BF16, name="elhs", tag="elhs", align_bytes=64)
+
+        def turn_ecoef():
+            et = psum.tile([P, B, P], BF16, name="et", tag="bank")
+            for b in range(B):
+                nc.tensor.transpose(et[:, b, :], ecoef[:, b, :], identb[:])
+            nc.scalar.copy(out=elhs[:], in_=et[:])
+
+        def load_lin2():
+            for b in range(B):
+                nc.sync.dma_start(
+                    out=erhs[LROW + TERMS * b : LROW + TERMS * (b + 1)].rearrange("p y o -> p (y o)"),
+                    in_=lin2[b].rearrange("y o -> (y o)").partition_broadcast(TERMS),
+                )
+
+        def fill_e(h):
+            ex = work.tile([P, HALF, L, OGRP], F32, name="ex", tag="ex", bufs=3, align_bytes=64)
+            for c in range(HALF):
+                g = (h % 2) * HALF + c
+                eb = psum.tile([P, L, OGRP], F32, name="eb", tag="bank")
+                nc.tensor.matmul(eb[:], lhsT=elhs[:, h // 2, :], rhs=erhs[:, :, g * OGRP : (g + 1) * OGRP], start=True, stop=True)
+                nc.scalar.copy(out=ex[:, c], in_=eb[:])
+            exs[h] = ex
+
+        def pair_bank(b, g):
+            cols = slice(b * L, (b + 1) * L)
+            pb = psum.tile([P, OGRP, L], F32, name="pair", tag="bank")
+            for k in range(OGRP):
+                o = g * OGRP + k
+                nc.tensor.matmul_mx(
+                    out=pb[:, k, :],
+                    lhsT=tcod[:, o, cols].bitcast(FP8X4),
+                    lhsT_scale=tscl[:, o, cols],
+                    rhs=x2c[:, cols].bitcast(FP8X4),
+                    rhs_scale=x2s[:, cols],
+                    start=True,
+                    stop=True,
+                )
+            return pb
+
+        def mix(b, g, pb, stage, ysl):
+            nc.vector.scalar_tensor_tensor(
+                out=stage[:, ysl, g * OGRP : (g + 1) * OGRP],
+                in0=pb[:, :, ysl].rearrange("p k y -> p y k"),
+                scalar=bwn[:, 0:1],
+                in1=exs[2 * b + g // HALF][:, g % HALF, ysl, :],
+                op0=ALU.mult,
+                op1=ALU.add,
+            )
+
+        def new_stage():
+            return work.tile([P, L, O], F32, name="stage", tag="tb", bufs=2, align_bytes=64)
+
         with tc.manual_schedule(engines={mybir.EngineType.DVE}):
             for i in range(NP + 2):
                 for o in (OP * (i + 2), OP * (i + 2) + 1):
@@ -218,10 +294,13 @@ def tile_biaffine_pa_kernel(tc, x1, x2, bw, W_bil, t_ones, lin1, lin2, b_lin, ou
                         load_w(o)
                 if i % 2 == 0 and i // 2 + 1 < O // OGRP:
                     load_bias(i // 2 + 1)
-                if NP - 8 <= i < NP and i % 2 == 0:
-                    load_lin2((i - (NP - 8)) // 2)
                 if i == 1:
                     quant_tokens("x2", x2c[:], x2s[:])
+                if i == E_STEP:
+                    load_lin2()
+                    turn_ecoef()
+                if i == NP - 2:
+                    fill_e(0)
                 if 0 <= i - 1 < NP:
                     copy_out(i - 1, [])
                 if 0 <= i - 2:
@@ -233,55 +312,34 @@ def tile_biaffine_pa_kernel(tc, x1, x2, bw, W_bil, t_ones, lin1, lin2, b_lin, ou
                 if i < NP:
                     add_bias(i)
                     transposes(i, OP)
+                if i == NP:
+                    stage = new_stage()
+                if i >= NP:
+                    for g in range((i - NP) * HALF, (i - NP + 1) * HALF):
+                        mix(0, g, pair_bank(0, g), stage, slice(0, L))
+                    fill_e(i - NP + 1)
+                if i == NP + 1:
+                    fill_e(3)
+                    fill_e(4)
                 if i + 2 < NP:
                     interleave_w(i + 2, C_SPLIT, G_SPLIT)
 
-        def add_lin2(b, stage, tmps, g, ysl):
-            osl = slice(g * OGRP, (g + 1) * OGRP)
-            nc.vector.scalar_tensor_tensor(
-                out=stage[:, ysl, osl],
-                in0=lin2bs[b][:, ysl, osl],
-                scalar=bwn[:, 1:2],
-                in1=tmps[g][:, :, ysl].rearrange("p k y -> p y k"),
-                op0=ALU.mult,
-                op1=ALU.add,
-            )
-
-        for b in range(B):
-            cols = slice(b * L, (b + 1) * L)
-            stage = work.tile([P, L, O], F32, name="stage", tag="tb", bufs=2, align_bytes=64)
-            tmps = []
+        nc.sync.dma_start(out=out[0], in_=stage[:])
+        for b in range(1, B):
+            stage = new_stage()
+            pbs = []
             for g in range(O // OGRP):
-                pb = psum.tile([P, OGRP, L], F32, name="pair", tag="bank")
-                for k in range(OGRP):
-                    o = g * OGRP + k
-                    nc.tensor.matmul_mx(
-                        out=pb[:, k, :],
-                        lhsT=tcod[:, o, cols].bitcast(FP8X4),
-                        lhsT_scale=tscl[:, o, cols],
-                        rhs=x2c[:, cols].bitcast(FP8X4),
-                        rhs_scale=x2s[:, cols],
-                        start=True,
-                        stop=True,
-                    )
-                if g % 4 == 0:
-                    tmp4 = work.tile([P, 4, OGRP, L], F32, name="tmp4", tag="tg", bufs=2, align_bytes=64)
-                tmp = tmp4[:, g % 4]
-                for k in range(OGRP):
-                    o = g * OGRP + k
-                    xcol = xterm[:, b * O + o : b * O + o + 1]
-                    if o % V_READ_EVERY == V_READ_EVERY - 1:
-                        nc.vector.tensor_scalar(out=tmp[:, k, :], in0=pb[:, k, :], scalar1=bwn[:, 0:1], scalar2=xcol, op0=ALU.mult, op1=ALU.add)
-                    else:
-                        nc.scalar.activation(out=tmp[:, k, :], in_=pb[:, k, :], func=ACT.Identity, bias=xcol, scale=bwn[:, 0:1])
-                tmps.append(tmp)
+                pbs.append(pair_bank(b, g))
                 if b < B - 1:
-                    add_lin2(b, stage, tmps, g, slice(0, L))
+                    mix(b, g, pbs[g], stage, slice(0, L))
+                    h = 2 * b + g // HALF + 3
+                    if g % HALF == HALF - 1 and h < 2 * B:
+                        fill_e(h)
             if b < B - 1:
                 nc.sync.dma_start(out=out[b], in_=stage[:])
             else:
                 for y0 in range(0, L, YH):
                     ysl = slice(y0, y0 + YH)
                     for g in range(O // OGRP):
-                        add_lin2(b, stage, tmps, g, ysl)
+                        mix(b, g, pbs[g], stage, ysl)
                     nc.sync.dma_start(out=out[b, :, ysl, :], in_=stage[:, ysl, :])

@@ -16,44 +16,35 @@ ACT = mybir.ActivationFunctionType
 
 P = 128
 PACK = 4
-BANK_DT = BF16
 OGRP = 4
+NG = O // OGRP
 YH = 64
 RUN = 16
 TERMS = 3
-E_STEP = 3
 LROW = TERMS * O
-HALF = O // OGRP // 2
 W_BUFS = 6
 C_SPLIT = 84
 G_SPLIT = 84
+C_SPLIT0 = 52
 OP = 2
 NP = O // OP
+X2_STEP = 4
+C_STEP = 2
+L_STEP = 7
+LEAD = 4
+EARLY = 1
+TAIL = 1
+LAG = 3
+T_AT = {0: NP - 2, 3: NP - 1}
 
 
 def tile_biaffine_pa_kernel(tc, x1, x2, bw, W_bil, t_ones, lin1, lin2, b_lin, out):
     nc = tc.nc
     with ExitStack() as ctx:
         keep = ctx.enter_context(tc.tile_pool(name="keep", bufs=1))
-        work = ctx.enter_context(tc.tile_pool(name="work", bufs=2))
+        group = ctx.enter_context(tc.tile_pool(name="group", bufs=4))
         psum = ctx.enter_context(tc.psum_pool(name="psum", bufs=8))
-
-        bw_sb = keep.tile([P, 2], BF16, name="bw_sb", tag="bw_sb")
-        nc.scalar.dma_start(out=bw_sb[:], in_=bw.partition_broadcast(P))
-        bl_sb = keep.tile([P, O], BF16, name="bl_sb", tag="bl_sb")
-        nc.scalar.dma_start(out=bl_sb[:], in_=b_lin.partition_broadcast(P))
-        t1_sb = keep.tile([P, B, O], BF16, name="t1_sb", tag="t1_sb")
-        nc.scalar.dma_start(out=t1_sb[:], in_=t_ones.rearrange("b x o -> x b o"))
-        l1_sb = keep.tile([P, B, O], BF16, name="l1_sb", tag="l1_sb")
-        nc.scalar.dma_start(out=l1_sb[:], in_=lin1.rearrange("b x o -> x b o"))
-
-        warm = keep.tile([P, 1], F32, name="warm", tag="warm")
-        nc.vector.memset(warm[:], 0.0)
-        warm2 = keep.tile([P, 1], F32, name="warm2", tag="warm2")
-        nc.scalar.activation(out=warm2[:], in_=warm[:], func=ACT.Exp)
-
-        ident = keep.tile([P, P], F32, name="ident", tag="ident")
-        make_identity(nc, ident[:])
+        ctx.enter_context(tc.manual_schedule())
 
         x1c = keep.tile([P, B * L], U32, name="x1c", tag="x1c", align_bytes=64)
         x1s = keep.tile([P, B * L], U8, name="x1s", tag="x1s", align_bytes=64)
@@ -61,285 +52,314 @@ def tile_biaffine_pa_kernel(tc, x1, x2, bw, W_bil, t_ones, lin1, lin2, b_lin, ou
         x2s = keep.tile([P, B * L], U8, name="x2s", tag="x2s", align_bytes=64)
         tcod = keep.tile([P, O, B * L], U32, name="tcod", tag="tcod", align_bytes=64)
         tscl = keep.tile([P, O, B * L], U8, name="tscl", tag="tscl", align_bytes=64)
-
-        wraw, wgrp, wq, banks, tbs, xts, tgs, biases, exs = {}, {}, {}, {}, {}, {}, {}, {}, {}
-
-        def load_tokens(x, key):
-            raw = work.tile([P, B, D], BF16, name="xraw", tag="wraw", bufs=W_BUFS, align_bytes=64)
-            for b in range(B):
-                nc.sync.dma_start(out=raw[:, b, :], in_=x[b])
-            tbs[key] = raw
-
-        def load_w(o):
-            raw = work.tile([P, PACK, D], BF16, name="wraw", tag="wraw", bufs=W_BUFS, align_bytes=64)
-            nc.sync.dma_start(out=raw[:], in_=W_bil[o, 0:D, :].rearrange("(p s) j -> p s j", s=PACK))
-            wraw[o] = raw
-
-        def load_bias(c):
-            bt = work.tile([P, OGRP, D], BF16, name="bias", tag="bias", bufs=2)
-            nc.sync.dma_start(out=bt[:], in_=W_bil[c * OGRP : (c + 1) * OGRP, D, :].partition_broadcast(P))
-            biases[c] = bt
-
-        def interleave_w(i, c_split, g_split):
-            g = work.tile([P, OP * D, PACK], BF16, name="wgrp", tag="wgrp", bufs=2, align_bytes=64)
-            for q in range(OP):
-                dst = g[:].rearrange("p (q c t) s -> p q c s t", q=OP, t=4)[:, q]
-                src = wraw[OP * i + q][:].rearrange("p s (c t) -> p c s t", t=4)
-                nc.scalar.copy(out=dst[:, 0:c_split], in_=src[:, 0:c_split])
-                if c_split < g_split:
-                    nc.vector.tensor_copy(out=dst[:, c_split:g_split], in_=src[:, c_split:g_split])
-                if g_split < P:
-                    nc.gpsimd.tensor_scalar(out=dst[:, g_split:], in0=src[:, g_split:], scalar1=1.0, scalar2=0.0, op0=ALU.mult, op1=ALU.add)
-            wgrp[i] = g
-
-        def quant_w(i):
-            wc = work.tile([P, OP * D], U32, name="wc", tag="wc", bufs=2, align_bytes=64)
-            ws = work.tile([P, OP * D], U8, name="ws", tag="ws", bufs=2, align_bytes=64)
-            nc.vector.quantize_mx(out=wc[:].bitcast(FP8X4), scales=ws[:], in_=wgrp[i][:].rearrange("p j s -> p (j s)"))
-            wq[i] = (wc, ws)
-
-        def stage1(o):
-            wc, ws = wq[o]
-            banks[o] = []
-            for b in range(B):
-                cols = slice(b * L, (b + 1) * L)
-                bank = psum.tile([P, OP * D], BANK_DT, name="bank", tag="bank")
-                nc.tensor.matmul_mx(
-                    out=bank[:],
-                    lhsT=x1c[:, cols].bitcast(FP8X4),
-                    lhsT_scale=x1s[:, cols],
-                    rhs=wc[:].bitcast(FP8X4),
-                    rhs_scale=ws[:],
-                    start=True,
-                    stop=True,
-                )
-                banks[o].append(bank)
-
-        def add_bias(i):
-            tb = work.tile([P, B, OP * D], BF16, name="tb", tag="tb", bufs=2, align_bytes=64)
-            per = OGRP // OP
-            rows = biases[i // per][:].rearrange("p g d -> p (g d)")[:, (i % per) * OP * D : (i % per + 1) * OP * D]
-            for b in range(B):
-                nc.vector.tensor_tensor(
-                    out=tb[:, b, :].rearrange("p (u a r) -> p a u r", u=2, r=RUN),
-                    in0=rows.rearrange("p (a u r) -> p a u r", u=2, r=RUN),
-                    in1=banks[i][b][:].rearrange("p (a u r) -> p a u r", u=2, r=RUN),
-                    op=ALU.add,
-                )
-            tbs[i] = tb
-
-        def transposes(key, n_o):
-            words = tbs[key][:].bitcast(F32)
-            xts[key] = []
-            for q in range(max(n_o, 1)):
-                for r in range(2):
-                    xt = psum.tile([P, 2, 2, L], F32, name="xt", tag="bank")
-                    for h in range(2):
-                        for u in range(2):
-                            if key == "x1":
-                                sel = words[:, 2 * r + h, u : D // 2 : 2]
-                            elif key == "x2":
-                                sel = words[:, u, (2 * r + h) * P : (2 * r + h + 1) * P]
-                            else:
-                                sel = words[:, 2 * r + h, (u * OP + q) * P : (u * OP + q + 1) * P]
-                            nc.tensor.transpose(xt[:, h, u, :], sel, ident[:])
-                    xts[key].append(xt)
-
-        def copy_out(key, v_q):
-            n = len(xts[key])
-            tg = work.tile([P, n // 2 * B * L * PACK], BF16, name="tg", tag="tg", bufs=2, align_bytes=64)
-            gw = tg[:].bitcast(F32).rearrange("p (b x u) -> p b x u", b=n * 2, u=2)
-            for q in range(n):
-                src = xts[key][q][:].rearrange("p h u x -> p h x u")
-                if q in v_q:
-                    nc.vector.tensor_copy(out=gw[:, 2 * q : 2 * q + 2], in_=src)
-                else:
-                    nc.scalar.copy(out=gw[:, 2 * q : 2 * q + 2], in_=src)
-            tgs[key] = tg
-
-        def quant_tokens(key, codes, scales):
-            nc.vector.quantize_mx(out=codes.bitcast(FP8X4), scales=scales, in_=tgs[key][:])
-
-        def permute_x2():
-            x2p = keep.tile([P, 2, B * D // 2], BF16, name="x2p", tag="x2p", align_bytes=64)
-            nc.vector.tensor_copy(
-                out=x2p[:].rearrange("p u (n r) -> p n u r", r=RUN),
-                in_=tbs["x2"][:].rearrange("p b (a u r) -> p (b a) u r", u=2, r=RUN),
-            )
-            tbs["x2"] = x2p
-
-        load_tokens(x1, "x1")
-        load_w(0)
-        load_w(1)
-        load_bias(0)
-        load_tokens(x2, "x2")
-        load_w(2)
-        load_w(3)
-
-        bwf = keep.tile([P, 2], F32, name="bwf", tag="bwf")
-        nc.vector.tensor_copy(out=bwf[:], in_=bw_sb[:])
-        bmax = keep.tile([P, 1], F32, name="bmax", tag="bmax")
-        nc.vector.tensor_tensor(out=bmax[:], in0=bwf[:, 0:1], in1=bwf[:, 1:2], op=ALU.max)
-        nmax = keep.tile([P, 1], F32, name="nmax", tag="nmax")
-        nc.vector.tensor_scalar(out=nmax[:], in0=bmax[:], scalar1=-1.0, scalar2=None, op0=ALU.mult)
-        bexp = keep.tile([P, 2], F32, name="bexp", tag="bexp")
-        nc.scalar.activation(out=bexp[:], in_=bwf[:], func=ACT.Exp, bias=nmax[:], scale=1.0)
-        bsum = keep.tile([P, 1], F32, name="bsum", tag="bsum")
-        nc.vector.tensor_tensor(out=bsum[:], in0=bexp[:, 0:1], in1=bexp[:, 1:2], op=ALU.add)
-        brec = keep.tile([P, 1], F32, name="brec", tag="brec")
-        nc.vector.reciprocal(out=brec[:], in_=bsum[:])
-        bwn = keep.tile([P, 2], F32, name="bwn", tag="bwn")
-        nc.vector.tensor_scalar(out=bwn[:], in0=bexp[:], scalar1=brec[:], scalar2=None, op0=ALU.mult)
-
-        lsum = keep.tile([P, B, O], F32, name="lsum", tag="lsum")
-        nc.vector.tensor_tensor(out=lsum[:], in0=l1_sb[:], in1=bl_sb[:].unsqueeze(1).to_broadcast([P, B, O]), op=ALU.add)
-        lscl = keep.tile([P, B * O], F32, name="lscl", tag="lscl")
-        nc.vector.tensor_scalar(out=lscl[:], in0=lsum[:].rearrange("p b o -> p (b o)"), scalar1=bwn[:, 1:2], scalar2=None, op0=ALU.mult)
-        xterm = keep.tile([P, B * O], F32, name="xterm", tag="xterm")
-        nc.vector.scalar_tensor_tensor(out=xterm[:], in0=t1_sb[:].rearrange("p b o -> p (b o)"), scalar=bwn[:, 0:1], in1=lscl[:], op0=ALU.mult, op1=ALU.add)
-
-        fold = keep.tile([P, O], F32, name="fold", tag="fold")
-        nc.gpsimd.tensor_tensor(out=fold[:], in0=ident[:, 0:O], in1=ident[:, O : 2 * O], op=ALU.add)
-        fold3 = keep.tile([P, O], F32, name="fold3", tag="fold3")
-        nc.gpsimd.tensor_tensor(out=fold3[:], in0=fold[:], in1=ident[:, 2 * O : 3 * O], op=ALU.add)
-        erhs = keep.tile([P, L, O], BF16, name="erhs", tag="erhs", align_bytes=64)
-        nc.gpsimd.tensor_scalar(out=erhs[:], in0=fold3[:].unsqueeze(1).to_broadcast([P, L, O]), scalar1=1.0, scalar2=0.0, op0=ALU.mult, op1=ALU.add)
-
-        transposes("x1", 0)
-        copy_out("x1", [1])
-        interleave_w(0, P // 2, P)
-        quant_tokens("x1", x1c[:], x1s[:])
-        permute_x2()
-        transposes("x2", 0)
-        quant_w(0)
-        stage1(0)
-        interleave_w(1, C_SPLIT, G_SPLIT)
-        copy_out("x2", [])
-
-        ecoef = keep.tile([P, B, P], BF16, name="ecoef", tag="ecoef", align_bytes=64)
-        nc.vector.memset(ecoef[:], 0.0)
-        xrest = xterm
-        wrest = bwn[:, 1:2]
-        for t in range(TERMS):
-            xt_out = ecoef[:, :, t * O : (t + 1) * O]
-            wt_out = ecoef[:].rearrange("p b k -> p (b k)")[:, LROW + t : LROW + t + (B - 1) * (P + TERMS) + 1 : P + TERMS]
-            nc.vector.tensor_copy(out=xt_out, in_=xrest[:].rearrange("p (b o) -> p b o", b=B))
-            nc.vector.tensor_copy(out=wt_out, in_=wrest.to_broadcast([P, B]))
-            if t + 1 < TERMS:
-                xnext = keep.tile([P, B * O], F32, name="xrest%d" % t, tag="xrest%d" % t)
-                nc.vector.tensor_tensor(out=xnext[:].rearrange("p (b o) -> p b o", b=B), in0=xrest[:].rearrange("p (b o) -> p b o", b=B), in1=xt_out, op=ALU.subtract)
-                wnext = keep.tile([P, 1], F32, name="wrest%d" % t, tag="wrest%d" % t)
-                nc.vector.tensor_tensor(out=wnext[:], in0=wrest, in1=ecoef[:, 0, LROW + t : LROW + t + 1], op=ALU.subtract)
-                xrest = xnext
-                wrest = wnext[:]
+        bw_sb = keep.tile([P, 2], BF16, name="bw_sb", tag="bw_sb")
+        bl_sb = keep.tile([P, O], BF16, name="bl_sb", tag="bl_sb")
+        t1_sb = keep.tile([P, B, O], BF16, name="t1_sb", tag="t1_sb")
+        l1_sb = keep.tile([P, B, O], BF16, name="l1_sb", tag="l1_sb")
+        warm = keep.tile([P, 1], F32, name="warm", tag="warm")
+        warm2 = keep.tile([P, 1], F32, name="warm2", tag="warm2")
+        ident = keep.tile([P, P], F32, name="ident", tag="ident")
         identb = keep.tile([P, P], BF16, name="identb", tag="identb")
-        nc.vector.tensor_copy(out=identb[:], in_=ident[:])
+        ecoef = keep.tile([P, B, P], BF16, name="ecoef", tag="ecoef", align_bytes=64)
         elhs = keep.tile([P, B, P], BF16, name="elhs", tag="elhs", align_bytes=64)
+        fold = keep.tile([P, O], F32, name="fold", tag="fold")
+        fold3 = keep.tile([P, O], BF16, name="fold3", tag="fold3")
+        erhs = keep.tile([P, NG, L, OGRP], BF16, name="erhs", tag="erhs", align_bytes=64)
+        bwf = keep.tile([P, 2], F32, name="bwf", tag="bwf")
+        bmax = keep.tile([P, 1], F32, name="bmax", tag="bmax")
+        nmax = keep.tile([P, 1], F32, name="nmax", tag="nmax")
+        bexp = keep.tile([P, 2], F32, name="bexp", tag="bexp")
+        bsum = keep.tile([P, 1], F32, name="bsum", tag="bsum")
+        brec = keep.tile([P, 1], F32, name="brec", tag="brec")
+        bwn = keep.tile([P, 2], F32, name="bwn", tag="bwn")
+        lsum = keep.tile([P, B, O], F32, name="lsum", tag="lsum")
+        lscl = keep.tile([P, B * O], F32, name="lscl", tag="lscl")
+        xterm = keep.tile([P, B * O], F32, name="xterm", tag="xterm")
 
-        def turn_ecoef():
-            et = psum.tile([P, B, P], BF16, name="et", tag="bank")
-            for b in range(B):
-                nc.tensor.transpose(et[:, b, :], ecoef[:, b, :], identb[:])
-            nc.scalar.copy(out=elhs[:], in_=et[:])
+        wraw, wgrp, wq, banks, tbs, xts, tgs, biases, exs, rests, stages, pairs = {}, {}, {}, {}, {}, {}, {}, {}, {}, {}, {}, {}
 
-        def load_lin2():
-            for b in range(B):
-                nc.sync.dma_start(
-                    out=erhs[LROW + TERMS * b : LROW + TERMS * (b + 1)].rearrange("p y o -> p (y o)"),
-                    in_=lin2[b].rearrange("y o -> (y o)").partition_broadcast(TERMS),
+        with tc.tile_pool(name="work", bufs=2) as work:
+            def load_tokens(x, key, tag, bufs):
+                raw = group.tile([P, B, D], BF16, name="xraw", tag=tag, bufs=bufs, align_bytes=64)
+                for b in range(0, B, 2):
+                    nc.sync.dma_start(out=raw[:, b : b + 2, :], in_=x[b : b + 2].rearrange("b x i -> x b i"))
+                tbs[key] = raw
+
+            def load_w(o):
+                raw = work.tile([P, PACK, D], BF16, name="wraw", tag="wraw", bufs=W_BUFS, align_bytes=64)
+                nc.sync.dma_start(out=raw[:], in_=W_bil[o, 0:D, :].rearrange("(p s) j -> p s j", s=PACK))
+                wraw[o] = raw
+
+            def load_bias(c):
+                bt = work.tile([P, OGRP, D], BF16, name="bias", tag="bias", bufs=3)
+                nc.sync.dma_start(out=bt[:], in_=W_bil[c * OGRP : (c + 1) * OGRP, D, :].partition_broadcast(P))
+                biases[c] = bt
+
+            def interleave_w(i, c_split, g_split):
+                g = work.tile([P, OP * D, PACK], BF16, name="wgrp", tag="wgrp", bufs=2, align_bytes=64)
+                for q in range(OP):
+                    dst = g[:].rearrange("p (q c t) s -> p q c s t", q=OP, t=4)[:, q]
+                    src = wraw[OP * i + q][:].rearrange("p s (c t) -> p c s t", t=4)
+                    nc.scalar.copy(out=dst[:, 0:c_split], in_=src[:, 0:c_split])
+                    if c_split < g_split:
+                        nc.vector.tensor_copy(out=dst[:, c_split:g_split], in_=src[:, c_split:g_split])
+                    nc.gpsimd.tensor_scalar(out=dst[:, g_split:], in0=src[:, g_split:], scalar1=1.0, scalar2=0.0, op0=ALU.mult, op1=ALU.add)
+                wgrp[i] = g
+
+            def quant_w(i):
+                wc = work.tile([P, OP * D], U32, name="wc", tag="wc", bufs=2, align_bytes=64)
+                ws = work.tile([P, OP * D], U8, name="ws", tag="ws", bufs=2, align_bytes=64)
+                nc.vector.quantize_mx(out=wc[:].bitcast(FP8X4), scales=ws[:], in_=wgrp[i][:].rearrange("p j s -> p (j s)"))
+                wq[i] = (wc, ws)
+
+            def stage1(i):
+                wc, ws = wq[i]
+                banks[i] = []
+                for b in range(B):
+                    cols = slice(b * L, (b + 1) * L)
+                    bank = psum.tile([P, OP * D], BF16, name="bank", tag="bank")
+                    nc.tensor.matmul_mx(
+                        out=bank[:],
+                        lhsT=x1c[:, cols].bitcast(FP8X4),
+                        lhsT_scale=x1s[:, cols],
+                        rhs=wc[:].bitcast(FP8X4),
+                        rhs_scale=ws[:],
+                        start=True,
+                        stop=True,
+                    )
+                    banks[i].append(bank)
+
+            def add_bias(i):
+                tb = work.tile([P, B, OP * D], BF16, name="tb", tag="tb", bufs=2, align_bytes=64)
+                per = OGRP // OP
+                rows = biases[i // per][:].rearrange("p g d -> p (g d)")[:, (i % per) * OP * D : (i % per + 1) * OP * D]
+                for b in range(B):
+                    nc.vector.tensor_tensor(
+                        out=tb[:, b, :].rearrange("p (u a r) -> p a u r", u=2, r=RUN),
+                        in0=rows.rearrange("p (a u r) -> p a u r", u=2, r=RUN),
+                        in1=banks[i][b][:].rearrange("p (a u r) -> p a u r", u=2, r=RUN),
+                        op=ALU.add,
+                    )
+                tbs[i] = tb
+
+            def transposes(key, n):
+                words = tbs[key][:].bitcast(F32)
+                xts[key] = []
+                for q in range(n):
+                    for r in range(2):
+                        xt = psum.tile([P, 2, 2, L], F32, name="xt", tag="bank")
+                        for h in range(2):
+                            for u in range(2):
+                                if key == "x1":
+                                    sel = words[:, 2 * r + h, u : D // 2 : 2]
+                                elif key == "x2":
+                                    sel = words[:, u, (2 * r + h) * P : (2 * r + h + 1) * P]
+                                else:
+                                    sel = words[:, 2 * r + h, (u * OP + q) * P : (u * OP + q + 1) * P]
+                                nc.tensor.transpose(xt[:, h, u, :], sel, ident[:])
+                        xts[key].append(xt)
+
+            def grouped(key, tag, bufs):
+                tgs[key] = group.tile([P, len(xts[key]) * 2 * L * PACK], BF16, name="tg", tag=tag, bufs=bufs, align_bytes=64)
+
+            def copy_out(key, copy, qs):
+                gw = tgs[key][:].bitcast(F32).rearrange("p (b x u) -> p b x u", x=L, u=2)
+                for q in qs:
+                    copy(out=gw[:, 2 * q : 2 * q + 2], in_=xts[key][q][:].rearrange("p h u x -> p h x u"))
+
+            def quant_tokens(key, codes, scales):
+                nc.vector.quantize_mx(out=codes.bitcast(FP8X4), scales=scales, in_=tgs[key][:])
+
+            def quant_t(i):
+                osl = slice(OP * i, OP * (i + 1))
+                quant_tokens(i, tcod[:, osl, :].rearrange("p o n -> p (o n)"), tscl[:, osl, :].rearrange("p o n -> p (o n)"))
+
+            def permute_x2():
+                x2p = group.tile([P, 2, B * D // 2], BF16, name="x2p", tag="tg", bufs=4, align_bytes=64)
+                nc.vector.tensor_copy(
+                    out=x2p[:].rearrange("p u (n r) -> p n u r", r=RUN),
+                    in_=tbs["x2"][:].rearrange("p b (a u r) -> p (b a) u r", u=2, r=RUN),
                 )
+                tbs["x2"] = x2p
 
-        def fill_e(h):
-            ex = work.tile([P, HALF, L, OGRP], F32, name="ex", tag="ex", bufs=3, align_bytes=64)
-            for c in range(HALF):
-                g = (h % 2) * HALF + c
+            def split_ecoef(t):
+                xrest, wrest = rests[t]
+                xt_out = ecoef[:, :, t * O : (t + 1) * O]
+                wt_out = ecoef[:].rearrange("p b k -> p (b k)")[:, LROW + t : LROW + t + (B - 1) * (P + TERMS) + 1 : P + TERMS]
+                nc.gpsimd.tensor_copy(out=xt_out, in_=xrest[:].rearrange("p (b o) -> p b o", b=B))
+                nc.gpsimd.tensor_copy(out=wt_out, in_=wrest.to_broadcast([P, B]))
+                if t + 1 < TERMS:
+                    xnext = keep.tile([P, B * O], F32, name="xrest%d" % t, tag="xrest%d" % t)
+                    nc.gpsimd.tensor_tensor(out=xnext[:].rearrange("p (b o) -> p b o", b=B), in0=xrest[:].rearrange("p (b o) -> p b o", b=B), in1=xt_out, op=ALU.subtract)
+                    wnext = keep.tile([P, 1], F32, name="wrest%d" % t, tag="wrest%d" % t)
+                    nc.gpsimd.tensor_tensor(out=wnext[:], in0=wrest, in1=ecoef[:, 0, LROW + t : LROW + t + 1], op=ALU.subtract)
+                    rests[t + 1] = (xnext, wnext[:])
+
+            def turn_ecoef():
+                et = psum.tile([P, B, P], BF16, name="et", tag="bank")
+                for b in range(B):
+                    nc.tensor.transpose(et[:, b, :], ecoef[:, b, :], identb[:])
+                nc.scalar.copy(out=elhs[:], in_=et[:])
+
+            def load_lin2():
+                lrow = group.tile([P, L, O], BF16, name="lrow", tag="tg", bufs=4, align_bytes=64)
+                for b in range(B):
+                    nc.sync.dma_start(
+                        out=lrow[LROW + TERMS * b : LROW + TERMS * (b + 1)].rearrange("p y o -> p (y o)"),
+                        in_=lin2[b].rearrange("y o -> (y o)").partition_broadcast(TERMS),
+                    )
+                tbs["lin2"] = lrow
+
+            def place_lin2():
+                rows = slice(LROW, LROW + TERMS * B)
+                nc.vector.tensor_copy(out=erhs[rows], in_=tbs["lin2"][rows].rearrange("p y (g k) -> p g y k", k=OGRP))
+
+            def fill_e(n):
+                if n % 4 == 0:
+                    exs[n // 4] = group.tile([P, 4, L, OGRP], F32, name="ex", tag="tg", bufs=4, align_bytes=64)
                 eb = psum.tile([P, L, OGRP], F32, name="eb", tag="bank")
-                nc.tensor.matmul(eb[:], lhsT=elhs[:, h // 2, :], rhs=erhs[:, :, g * OGRP : (g + 1) * OGRP], start=True, stop=True)
-                nc.scalar.copy(out=ex[:, c], in_=eb[:])
-            exs[h] = ex
+                nc.tensor.matmul(eb[:].rearrange("p y k -> p (y k)"), lhsT=elhs[:, n // NG, :], rhs=erhs[:, n % NG].rearrange("p y k -> p (y k)"), start=True, stop=True)
+                nc.scalar.copy(out=exs[n // 4][:, n % 4], in_=eb[:])
 
-        def pair_bank(b, g):
-            cols = slice(b * L, (b + 1) * L)
-            pb = psum.tile([P, OGRP, L], F32, name="pair", tag="bank")
-            for k in range(OGRP):
-                o = g * OGRP + k
-                nc.tensor.matmul_mx(
-                    out=pb[:, k, :],
-                    lhsT=tcod[:, o, cols].bitcast(FP8X4),
-                    lhsT_scale=tscl[:, o, cols],
-                    rhs=x2c[:, cols].bitcast(FP8X4),
-                    rhs_scale=x2s[:, cols],
-                    start=True,
-                    stop=True,
+            def pair_bank(n):
+                b, g = divmod(n, NG)
+                cols = slice(b * L, (b + 1) * L)
+                pb = psum.tile([P, OGRP, L], F32, name="pair", tag="bank")
+                for k in range(OGRP):
+                    o = g * OGRP + k
+                    nc.tensor.matmul_mx(
+                        out=pb[:, k, :],
+                        lhsT=tcod[:, o, cols].bitcast(FP8X4),
+                        lhsT_scale=tscl[:, o, cols],
+                        rhs=x2c[:, cols].bitcast(FP8X4),
+                        rhs_scale=x2s[:, cols],
+                        start=True,
+                        stop=True,
+                    )
+                pairs[n] = pb
+
+            def mix(n, ysl):
+                b, g = divmod(n, NG)
+                if b not in stages:
+                    stages[b] = late.tile([P, L, O], F32, name="stage", tag="stage", bufs=B, align_bytes=64)
+                nc.vector.scalar_tensor_tensor(
+                    out=stages[b][:, ysl, g * OGRP : (g + 1) * OGRP],
+                    in0=pairs[n][:, :, ysl].rearrange("p k y -> p y k"),
+                    scalar=bwn[:, 0:1],
+                    in1=exs[n // 4][:, n % 4, ysl, :],
+                    op0=ALU.mult,
+                    op1=ALU.add,
                 )
-            return pb
 
-        def mix(b, g, pb, stage, ysl):
-            nc.vector.scalar_tensor_tensor(
-                out=stage[:, ysl, g * OGRP : (g + 1) * OGRP],
-                in0=pb[:, :, ysl].rearrange("p k y -> p y k"),
-                scalar=bwn[:, 0:1],
-                in1=exs[2 * b + g // HALF][:, g % HALF, ysl, :],
-                op0=ALU.mult,
-                op1=ALU.add,
+            nc.scalar.dma_start(out=bw_sb[:], in_=bw.partition_broadcast(P))
+            nc.scalar.dma_start(out=bl_sb[:], in_=b_lin.partition_broadcast(P))
+            nc.scalar.dma_start(out=t1_sb[:], in_=t_ones.rearrange("b x o -> x b o"))
+            nc.scalar.dma_start(out=l1_sb[:], in_=lin1.rearrange("b x o -> x b o"))
+            load_w(0)
+            load_tokens(x1, "x1", "tg", 4)
+            load_w(1)
+            load_w(2)
+            load_w(3)
+            load_w(4)
+            load_w(5)
+            load_bias(0)
+
+            make_identity(nc, ident[:])
+            nc.gpsimd.tensor_copy(out=identb[:], in_=ident[:])
+            nc.gpsimd.memset(ecoef[:], 0.0)
+
+            nc.vector.memset(warm[:], 0.0)
+            nc.scalar.activation(out=warm2[:], in_=warm[:], func=ACT.Exp)
+            nc.vector.tensor_tensor(out=fold[:], in0=ident[:, 0:O], in1=ident[:, O : 2 * O], op=ALU.add)
+            nc.vector.tensor_tensor(out=fold3[:], in0=fold[:], in1=ident[:, 2 * O : 3 * O], op=ALU.add)
+            nc.vector.tensor_copy(
+                out=erhs[:],
+                in_=fold3[:].rearrange("p (g k) -> p g k", k=OGRP).unsqueeze(2).to_broadcast([P, NG, L, OGRP]),
             )
+            nc.vector.tensor_copy(out=bwf[:], in_=bw_sb[:])
+            nc.vector.tensor_tensor(out=bmax[:], in0=bwf[:, 0:1], in1=bwf[:, 1:2], op=ALU.max)
+            nc.vector.tensor_scalar(out=nmax[:], in0=bmax[:], scalar1=-1.0, scalar2=None, op0=ALU.mult)
 
-        def new_stage():
-            return work.tile([P, L, O], F32, name="stage", tag="tb", bufs=2, align_bytes=64)
+            nc.scalar.activation(out=bexp[:], in_=bwf[:], func=ACT.Exp, bias=nmax[:], scale=1.0)
+            nc.vector.tensor_tensor(out=bsum[:], in0=bexp[:, 0:1], in1=bexp[:, 1:2], op=ALU.add)
+            nc.vector.tensor_tensor(out=lsum[:], in0=l1_sb[:], in1=bl_sb[:].unsqueeze(1).to_broadcast([P, B, O]), op=ALU.add)
+            nc.vector.reciprocal(out=brec[:], in_=bsum[:])
+            nc.vector.tensor_scalar(out=bwn[:], in0=bexp[:], scalar1=brec[:], scalar2=None, op0=ALU.mult)
+            nc.vector.tensor_scalar(out=lscl[:], in0=lsum[:].rearrange("p b o -> p (b o)"), scalar1=bwn[:, 1:2], scalar2=None, op0=ALU.mult)
+            nc.vector.scalar_tensor_tensor(out=xterm[:], in0=t1_sb[:].rearrange("p b o -> p (b o)"), scalar=bwn[:, 0:1], in1=lscl[:], op0=ALU.mult, op1=ALU.add)
+            rests[0] = (xterm, bwn[:, 1:2])
 
-        with tc.manual_schedule(engines={mybir.EngineType.DVE}):
-            for i in range(NP + 2):
-                for o in (OP * (i + 2), OP * (i + 2) + 1):
+            transposes("x1", 1)
+            interleave_w(0, C_SPLIT0, G_SPLIT)
+            grouped("x1", "tgx", 1)
+            copy_out("x1", nc.vector.tensor_copy, [0, 1])
+            quant_w(0)
+            quant_tokens("x1", x1c[:], x1s[:])
+            stage1(0)
+            interleave_w(1, C_SPLIT, G_SPLIT)
+
+            full = slice(0, L)
+            for i in range(NP + 1):
+                for o in (OP * (i + 3), OP * (i + 3) + 1):
                     if o < O:
                         load_w(o)
                 if i % 2 == 0 and i // 2 + 1 < O // OGRP:
                     load_bias(i // 2 + 1)
-                if i == 1:
-                    quant_tokens("x2", x2c[:], x2s[:])
-                if i == E_STEP:
+                if i == X2_STEP - 2:
+                    load_tokens(x2, "x2", "tg", 4)
+                if i == L_STEP:
                     load_lin2()
+
+                if i + 2 < NP and i <= EARLY:
+                    interleave_w(i + 2, C_SPLIT, G_SPLIT)
+                v_words = [1, 3] if i > NP - TAIL else []
+                if i >= 1:
+                    grouped(i - 1, "tg", 4)
+                    copy_out(i - 1, nc.scalar.copy, [q for q in range(4) if q not in v_words])
+                if i == C_STEP + TERMS + 1:
                     turn_ecoef()
-                if i == NP - 2:
-                    fill_e(0)
-                if 0 <= i - 1 < NP:
-                    copy_out(i - 1, [])
-                if 0 <= i - 2:
-                    osl = slice(OP * (i - 2), OP * (i - 1))
-                    quant_tokens(i - 2, tcod[:, osl, :].rearrange("p o n -> p (o n)"), tscl[:, osl, :].rearrange("p o n -> p (o n)"))
+                if i == NP - 1:
+                    for n in range(LEAD):
+                        fill_e(n)
+
+                if i >= LAG:
+                    quant_t(i - LAG)
                 if i + 1 < NP:
                     quant_w(i + 1)
                     stage1(i + 1)
+                if v_words:
+                    copy_out(i - 1, nc.vector.tensor_copy, v_words)
                 if i < NP:
                     add_bias(i)
-                    transposes(i, OP)
-                if i == NP:
-                    stage = new_stage()
-                if i >= NP:
-                    for g in range((i - NP) * HALF, (i - NP + 1) * HALF):
-                        mix(0, g, pair_bank(0, g), stage, slice(0, L))
-                    fill_e(i - NP + 1)
-                if i == NP + 1:
-                    fill_e(3)
-                    fill_e(4)
-                if i + 2 < NP:
+                    transposes(i, 2)
+                if i == X2_STEP:
+                    permute_x2()
+                    transposes("x2", 1)
+                if i == X2_STEP + 1:
+                    grouped("x2", "tgx", 1)
+                    copy_out("x2", nc.vector.tensor_copy, [0, 1])
+                if i == X2_STEP + 3:
+                    quant_tokens("x2", x2c[:], x2s[:])
+                if i == L_STEP + 3:
+                    place_lin2()
+                if i + 2 < NP and i > EARLY:
                     interleave_w(i + 2, C_SPLIT, G_SPLIT)
+                if C_STEP <= i < C_STEP + TERMS:
+                    split_ecoef(i - C_STEP)
 
-        nc.sync.dma_start(out=out[0], in_=stage[:])
-        for b in range(1, B):
-            stage = new_stage()
-            pbs = []
-            for g in range(O // OGRP):
-                pbs.append(pair_bank(b, g))
-                if b < B - 1:
-                    mix(b, g, pbs[g], stage, slice(0, L))
-                    h = 2 * b + g // HALF + 3
-                    if g % HALF == HALF - 1 and h < 2 * B:
-                        fill_e(h)
-            if b < B - 1:
-                nc.sync.dma_start(out=out[b], in_=stage[:])
-            else:
-                for y0 in range(0, L, YH):
-                    ysl = slice(y0, y0 + YH)
-                    for g in range(O // OGRP):
-                        mix(b, g, pbs[g], stage, ysl)
-                    nc.sync.dma_start(out=out[b, :, ysl, :], in_=stage[:, ysl, :])
+        late = ctx.enter_context(tc.tile_pool(name="late", bufs=B))
+        for n in range(B * NG):
+            if n in T_AT:
+                quant_t(T_AT[n])
+            pair_bank(n)
+            if n + LEAD < B * NG:
+                fill_e(n + LEAD)
+            if n < (B - 1) * NG:
+                mix(n, full)
+                if n % NG == NG - 1:
+                    nc.sync.dma_start(out=out[n // NG], in_=stages[n // NG][:])
+        for y0 in range(0, L, YH):
+            ysl = slice(y0, y0 + YH)
+            for n in range((B - 1) * NG, B * NG):
+                mix(n, ysl)
+            nc.sync.dma_start(out=out[B - 1, :, ysl, :], in_=stages[B - 1][:, ysl, :])

@@ -19,20 +19,25 @@ PACK = 4
 OGRP = 4
 NG = O // OGRP
 YH = 64
+YE = L // NG
 RUN = 16
 TERMS = 3
 LROW = TERMS * O
 W_BUFS = 6
-C_SPLIT = 84
-G_SPLIT = 84
-C_SPLIT0 = 52
+C_SPLIT = 90
+G_SPLIT = 90
+C_SPLIT0 = 84
+G_SPLIT0 = 84
+PE_GRP = 32
 OP = 2
 NP = O // OP
 X2_STEP = 4
 C_STEP = 2
 L_STEP = 7
-LEAD = 4
-EARLY = 1
+LEAD = 8
+W_GRP = 2
+E_STEPS = 2
+EARLY = 0
 TAIL = 1
 LAG = 3
 T_AT = {0: NP - 2, 3: NP - 1}
@@ -64,7 +69,7 @@ def tile_biaffine_pa_kernel(tc, x1, x2, bw, W_bil, t_ones, lin1, lin2, b_lin, ou
         elhs = keep.tile([P, B, P], BF16, name="elhs", tag="elhs", align_bytes=64)
         fold = keep.tile([P, O], F32, name="fold", tag="fold")
         fold3 = keep.tile([P, O], BF16, name="fold3", tag="fold3")
-        erhs = keep.tile([P, NG, L, OGRP], BF16, name="erhs", tag="erhs", align_bytes=64)
+        erhs = keep.tile([P, L, O], BF16, name="erhs", tag="erhs", align_bytes=64)
         bwf = keep.tile([P, 2], F32, name="bwf", tag="bwf")
         bmax = keep.tile([P, 1], F32, name="bmax", tag="bmax")
         nmax = keep.tile([P, 1], F32, name="nmax", tag="nmax")
@@ -76,7 +81,7 @@ def tile_biaffine_pa_kernel(tc, x1, x2, bw, W_bil, t_ones, lin1, lin2, b_lin, ou
         lscl = keep.tile([P, B * O], F32, name="lscl", tag="lscl")
         xterm = keep.tile([P, B * O], F32, name="xterm", tag="xterm")
 
-        wraw, wgrp, wq, banks, tbs, xts, tgs, biases, exs, rests, stages, pairs = {}, {}, {}, {}, {}, {}, {}, {}, {}, {}, {}, {}
+        wraw, wgrp, wq, banks, tbs, xts, tgs, biases, exs, rests, stages, pairs, turned = {}, {}, {}, {}, {}, {}, {}, {}, {}, {}, {}, {}, {}
 
         with tc.tile_pool(name="work", bufs=2) as work:
             def load_tokens(x, key, tag, bufs):
@@ -91,19 +96,34 @@ def tile_biaffine_pa_kernel(tc, x1, x2, bw, W_bil, t_ones, lin1, lin2, b_lin, ou
                 wraw[o] = raw
 
             def load_bias(c):
-                bt = work.tile([P, OGRP, D], BF16, name="bias", tag="bias", bufs=3)
+                bt = work.tile([P, OGRP, D], BF16, name="bias", tag="bias", bufs=2)
                 nc.sync.dma_start(out=bt[:], in_=W_bil[c * OGRP : (c + 1) * OGRP, D, :].partition_broadcast(P))
                 biases[c] = bt
 
+            def turn_w(i):
+                wp = psum.tile([P, OP, PE_GRP * 4 * PACK], BF16, name="wp", tag="bank")
+                for q in range(OP):
+                    nc.tensor.matmul(
+                        wp[:, q].rearrange("p (c t s) -> p c s t", t=4, s=PACK),
+                        lhsT=identb[:],
+                        rhs=wraw[OP * i + q][:].rearrange("p s (c t) -> p c s t", t=4)[:, 0:PE_GRP],
+                        start=True,
+                        stop=True,
+                    )
+                turned[i] = wp
+
             def interleave_w(i, c_split, g_split):
-                g = work.tile([P, OP * D, PACK], BF16, name="wgrp", tag="wgrp", bufs=2, align_bytes=64)
+                g = work.tile([P, OP * D, PACK], BF16, name="wgrp", tag="wgrp", bufs=W_GRP, align_bytes=64)
                 for q in range(OP):
                     dst = g[:].rearrange("p (q c t) s -> p q c s t", q=OP, t=4)[:, q]
                     src = wraw[OP * i + q][:].rearrange("p s (c t) -> p c s t", t=4)
-                    nc.scalar.copy(out=dst[:, 0:c_split], in_=src[:, 0:c_split])
+                    c0 = PE_GRP if i in turned else 0
+                    nc.scalar.copy(out=dst[:, c0:c_split], in_=src[:, c0:c_split])
                     if c_split < g_split:
                         nc.vector.tensor_copy(out=dst[:, c_split:g_split], in_=src[:, c_split:g_split])
                     nc.gpsimd.tensor_scalar(out=dst[:, g_split:], in0=src[:, g_split:], scalar1=1.0, scalar2=0.0, op0=ALU.mult, op1=ALU.add)
+                if i in turned:
+                    nc.scalar.copy(out=g[:].rearrange("p (q j) s -> p q (j s)", q=OP)[:, :, 0 : PE_GRP * 16], in_=turned[i][:])
                 wgrp[i] = g
 
             def quant_w(i):
@@ -201,25 +221,25 @@ def tile_biaffine_pa_kernel(tc, x1, x2, bw, W_bil, t_ones, lin1, lin2, b_lin, ou
                     nc.tensor.transpose(et[:, b, :], ecoef[:, b, :], identb[:])
                 nc.scalar.copy(out=elhs[:], in_=et[:])
 
-            def load_lin2():
-                lrow = group.tile([P, L, O], BF16, name="lrow", tag="tg", bufs=4, align_bytes=64)
-                for b in range(B):
-                    nc.sync.dma_start(
-                        out=lrow[LROW + TERMS * b : LROW + TERMS * (b + 1)].rearrange("p y o -> p (y o)"),
-                        in_=lin2[b].rearrange("y o -> (y o)").partition_broadcast(TERMS),
-                    )
-                tbs["lin2"] = lrow
-
-            def place_lin2():
-                rows = slice(LROW, LROW + TERMS * B)
-                nc.vector.tensor_copy(out=erhs[rows], in_=tbs["lin2"][rows].rearrange("p y (g k) -> p g y k", k=OGRP))
+            def load_lin2(b):
+                nc.sync.dma_start(
+                    out=erhs[LROW + TERMS * b : LROW + TERMS * (b + 1)].rearrange("p y o -> p (y o)"),
+                    in_=lin2[b].rearrange("y o -> (y o)").partition_broadcast(TERMS),
+                )
 
             def fill_e(n):
-                if n % 4 == 0:
-                    exs[n // 4] = group.tile([P, 4, L, OGRP], F32, name="ex", tag="tg", bufs=4, align_bytes=64)
-                eb = psum.tile([P, L, OGRP], F32, name="eb", tag="bank")
-                nc.tensor.matmul(eb[:].rearrange("p y k -> p (y k)"), lhsT=elhs[:, n // NG, :], rhs=erhs[:, n % NG].rearrange("p y k -> p (y k)"), start=True, stop=True)
-                nc.scalar.copy(out=exs[n // 4][:, n % 4], in_=eb[:])
+                b, c = divmod(n, NG)
+                if c == 0:
+                    if b:
+                        exs[b] = late.tile([P, L, O], F32, name="ex", tag="ex", bufs=2, align_bytes=64)
+                    else:
+                        exs[b] = group.tile([P, L, O], F32, name="ex0", tag="ex0", bufs=1, align_bytes=64)
+                ysl = slice(c * YE, (c + 1) * YE)
+                eb = psum.tile([P, YE, O], F32, name="eb", tag="bank")
+                nc.tensor.matmul(
+                    eb[:].rearrange("p y o -> p (y o)"), lhsT=elhs[:, b, :], rhs=erhs[:, ysl, :].rearrange("p y o -> p (y o)"), start=True, stop=True
+                )
+                nc.scalar.copy(out=exs[b][:, ysl, :], in_=eb[:])
 
             def pair_bank(n):
                 b, g = divmod(n, NG)
@@ -241,12 +261,12 @@ def tile_biaffine_pa_kernel(tc, x1, x2, bw, W_bil, t_ones, lin1, lin2, b_lin, ou
             def mix(n, ysl):
                 b, g = divmod(n, NG)
                 if b not in stages:
-                    stages[b] = late.tile([P, L, O], F32, name="stage", tag="stage", bufs=B, align_bytes=64)
+                    stages[b] = late.tile([P, L, O], F32, name="stage", tag="stage", bufs=3, align_bytes=64)
                 nc.vector.scalar_tensor_tensor(
                     out=stages[b][:, ysl, g * OGRP : (g + 1) * OGRP],
                     in0=pairs[n][:, :, ysl].rearrange("p k y -> p y k"),
                     scalar=bwn[:, 0:1],
-                    in1=exs[n // 4][:, n % 4, ysl, :],
+                    in1=exs[b][:, ysl, g * OGRP : (g + 1) * OGRP],
                     op0=ALU.mult,
                     op1=ALU.add,
                 )
@@ -272,10 +292,7 @@ def tile_biaffine_pa_kernel(tc, x1, x2, bw, W_bil, t_ones, lin1, lin2, b_lin, ou
             nc.scalar.activation(out=warm2[:], in_=warm[:], func=ACT.Exp)
             nc.vector.tensor_tensor(out=fold[:], in0=ident[:, 0:O], in1=ident[:, O : 2 * O], op=ALU.add)
             nc.vector.tensor_tensor(out=fold3[:], in0=fold[:], in1=ident[:, 2 * O : 3 * O], op=ALU.add)
-            nc.vector.tensor_copy(
-                out=erhs[:],
-                in_=fold3[:].rearrange("p (g k) -> p g k", k=OGRP).unsqueeze(2).to_broadcast([P, NG, L, OGRP]),
-            )
+            nc.vector.tensor_copy(out=erhs[:], in_=fold3[:].unsqueeze(1).to_broadcast([P, L, O]))
             nc.vector.tensor_copy(out=bwf[:], in_=bw_sb[:])
             nc.vector.tensor_tensor(out=bmax[:], in0=bwf[:, 0:1], in1=bwf[:, 1:2], op=ALU.max)
             nc.vector.tensor_scalar(out=nmax[:], in0=bmax[:], scalar1=-1.0, scalar2=None, op0=ALU.mult)
@@ -290,7 +307,7 @@ def tile_biaffine_pa_kernel(tc, x1, x2, bw, W_bil, t_ones, lin1, lin2, b_lin, ou
             rests[0] = (xterm, bwn[:, 1:2])
 
             transposes("x1", 1)
-            interleave_w(0, C_SPLIT0, G_SPLIT)
+            interleave_w(0, C_SPLIT0, G_SPLIT0)
             grouped("x1", "tgx", 1)
             copy_out("x1", nc.vector.tensor_copy, [0, 1])
             quant_w(0)
@@ -303,12 +320,12 @@ def tile_biaffine_pa_kernel(tc, x1, x2, bw, W_bil, t_ones, lin1, lin2, b_lin, ou
                 for o in (OP * (i + 3), OP * (i + 3) + 1):
                     if o < O:
                         load_w(o)
-                if i % 2 == 0 and i // 2 + 1 < O // OGRP:
+                if i % 2 == 1 and i // 2 + 1 < O // OGRP:
                     load_bias(i // 2 + 1)
                 if i == X2_STEP - 2:
                     load_tokens(x2, "x2", "tg", 4)
-                if i == L_STEP:
-                    load_lin2()
+                if L_STEP <= i < L_STEP + B:
+                    load_lin2(i - L_STEP)
 
                 if i + 2 < NP and i <= EARLY:
                     interleave_w(i + 2, C_SPLIT, G_SPLIT)
@@ -318,14 +335,16 @@ def tile_biaffine_pa_kernel(tc, x1, x2, bw, W_bil, t_ones, lin1, lin2, b_lin, ou
                     copy_out(i - 1, nc.scalar.copy, [q for q in range(4) if q not in v_words])
                 if i == C_STEP + TERMS + 1:
                     turn_ecoef()
-                if i == NP - 1:
-                    for n in range(LEAD):
+                if NP - E_STEPS <= i < NP:
+                    for n in range((i - NP + E_STEPS) * LEAD // E_STEPS, (i - NP + E_STEPS + 1) * LEAD // E_STEPS):
                         fill_e(n)
 
                 if i >= LAG:
                     quant_t(i - LAG)
                 if i + 1 < NP:
                     quant_w(i + 1)
+                    if i + 2 < NP and i >= 1:
+                        turn_w(i + 2)
                     stage1(i + 1)
                 if v_words:
                     copy_out(i - 1, nc.vector.tensor_copy, v_words)
@@ -340,8 +359,6 @@ def tile_biaffine_pa_kernel(tc, x1, x2, bw, W_bil, t_ones, lin1, lin2, b_lin, ou
                     copy_out("x2", nc.vector.tensor_copy, [0, 1])
                 if i == X2_STEP + 3:
                     quant_tokens("x2", x2c[:], x2s[:])
-                if i == L_STEP + 3:
-                    place_lin2()
                 if i + 2 < NP and i > EARLY:
                     interleave_w(i + 2, C_SPLIT, G_SPLIT)
                 if C_STEP <= i < C_STEP + TERMS:

@@ -104,9 +104,9 @@ def tile_biaffine_pa_kernel(tc, x1, x2, bw, W_bil, t_ones, lin1, lin2, b_lin, ou
                 wp = psum.tile([P, OP, PE_GRP * 4 * PACK], BF16, name="wp", tag="bank")
                 for q in range(OP):
                     nc.tensor.matmul(
-                        wp[:, q].rearrange("p (c t s) -> p c s t", t=4, s=PACK),
+                        wp[:, q].rearrange("p (j h e) -> p h j e", h=2, e=2),
                         lhsT=identb[:],
-                        rhs=wraw[OP * i + q][:].rearrange("p s (c t) -> p c s t", t=4)[:, 0:PE_GRP],
+                        rhs=wraw[OP * i + q][:, :, 0 : PE_GRP * 4].rearrange("p (h e) j -> p h j e", e=2),
                         start=True,
                         stop=True,
                     )

@@ -19,6 +19,8 @@ PACK = 4
 OGRP = 4
 NG = O // OGRP
 YH = 64
+HOLD = 6
+Y_CUTS = ((0, 64), (64, 128))
 YE = L // NG
 RUN = 16
 TERMS = 3
@@ -26,8 +28,14 @@ LROW = TERMS * O
 W_BUFS = 6
 C_SPLIT = 90
 G_SPLIT = 90
-C_SPLIT0 = 84
-G_SPLIT0 = 84
+C_SPLIT1 = 84
+G_SPLIT1 = 128
+C_SPLIT2 = 90
+G_SPLIT2 = 90
+ROUNDS = [0, 0, 1, 1, 1, 1, 1, 1, 1, 1, 1, 1, 1, 1, 1, 1]
+CS = [84, 88, 96]
+C_SPLIT0 = 64
+G_SPLIT0 = 128
 PE_GRP = 32
 OP = 2
 NP = O // OP
@@ -36,8 +44,9 @@ C_STEP = 2
 L_STEP = 7
 LEAD = 8
 W_GRP = 2
+EA = -1
 E_STEPS = 2
-EARLY = 0
+EARLY = 1
 TAIL = 1
 LAG = 3
 T_AT = {0: NP - 2, 3: NP - 1}
@@ -100,30 +109,36 @@ def tile_biaffine_pa_kernel(tc, x1, x2, bw, W_bil, t_ones, lin1, lin2, b_lin, ou
                 nc.sync.dma_start(out=bt[:], in_=W_bil[c * OGRP : (c + 1) * OGRP, D, :].partition_broadcast(P))
                 biases[c] = bt
 
+            def rounds(i):
+                return ROUNDS[i] if i < len(ROUNDS) else ROUNDS[-1]
+
             def turn_w(i):
-                wp = psum.tile([P, OP, PE_GRP * 4 * PACK], BF16, name="wp", tag="bank")
-                for q in range(OP):
+                turned[i] = []
+                for k in range(rounds(i)):
+                  wp = psum.tile([P, OP, PE_GRP * 4 * PACK], BF16, name="wp", tag="bank")
+                  for q in range(OP):
                     nc.tensor.matmul(
                         wp[:, q].rearrange("p (j h e) -> p h j e", h=2, e=2),
                         lhsT=identb[:],
-                        rhs=wraw[OP * i + q][:, :, 0 : PE_GRP * 4].rearrange("p (h e) j -> p h j e", e=2),
+                        rhs=wraw[OP * i + q][:, :, k * PE_GRP * 4 : (k + 1) * PE_GRP * 4].rearrange("p (h e) j -> p h j e", e=2),
                         start=True,
                         stop=True,
                     )
-                turned[i] = wp
+                  turned[i].append(wp)
 
             def interleave_w(i, c_split, g_split):
                 g = work.tile([P, OP * D, PACK], BF16, name="wgrp", tag="wgrp", bufs=W_GRP, align_bytes=64)
                 for q in range(OP):
                     dst = g[:].rearrange("p (q c t) s -> p q c s t", q=OP, t=4)[:, q]
                     src = wraw[OP * i + q][:].rearrange("p s (c t) -> p c s t", t=4)
-                    c0 = PE_GRP if i in turned else 0
+                    c0 = PE_GRP * len(turned.get(i, []))
                     nc.scalar.copy(out=dst[:, c0:c_split], in_=src[:, c0:c_split])
                     if c_split < g_split:
                         nc.vector.tensor_copy(out=dst[:, c_split:g_split], in_=src[:, c_split:g_split])
-                    nc.gpsimd.tensor_scalar(out=dst[:, g_split:], in0=src[:, g_split:], scalar1=1.0, scalar2=0.0, op0=ALU.mult, op1=ALU.add)
-                if i in turned:
-                    nc.scalar.copy(out=g[:].rearrange("p (q j) s -> p q (j s)", q=OP)[:, :, 0 : PE_GRP * 16], in_=turned[i][:])
+                    if g_split < P:
+                        nc.gpsimd.tensor_scalar(out=dst[:, g_split:], in0=src[:, g_split:], scalar1=1.0, scalar2=0.0, op0=ALU.mult, op1=ALU.add)
+                for k, wp in enumerate(turned.get(i, [])):
+                    nc.scalar.copy(out=g[:].rearrange("p (q j) s -> p q (j s)", q=OP)[:, :, k * PE_GRP * 16 : (k + 1) * PE_GRP * 16], in_=wp[:])
                 wgrp[i] = g
 
             def quant_w(i):
@@ -206,8 +221,8 @@ def tile_biaffine_pa_kernel(tc, x1, x2, bw, W_bil, t_ones, lin1, lin2, b_lin, ou
                 xrest, wrest = rests[t]
                 xt_out = ecoef[:, :, t * O : (t + 1) * O]
                 wt_out = ecoef[:].rearrange("p b k -> p (b k)")[:, LROW + t : LROW + t + (B - 1) * (P + TERMS) + 1 : P + TERMS]
-                nc.gpsimd.tensor_copy(out=xt_out, in_=xrest[:].rearrange("p (b o) -> p b o", b=B))
-                nc.gpsimd.tensor_copy(out=wt_out, in_=wrest.to_broadcast([P, B]))
+                nc.gpsimd.tensor_scalar(out=xt_out, in0=xrest[:].rearrange("p (b o) -> p b o", b=B), scalar1=1.0, scalar2=0.0, op0=ALU.mult, op1=ALU.add)
+                nc.gpsimd.tensor_scalar(out=wt_out, in0=wrest.to_broadcast([P, B]), scalar1=1.0, scalar2=0.0, op0=ALU.mult, op1=ALU.add)
                 if t + 1 < TERMS:
                     xnext = keep.tile([P, B * O], F32, name="xrest%d" % t, tag="xrest%d" % t)
                     nc.gpsimd.tensor_tensor(out=xnext[:].rearrange("p (b o) -> p b o", b=B), in0=xrest[:].rearrange("p (b o) -> p b o", b=B), in1=xt_out, op=ALU.subtract)
@@ -276,8 +291,8 @@ def tile_biaffine_pa_kernel(tc, x1, x2, bw, W_bil, t_ones, lin1, lin2, b_lin, ou
             nc.scalar.dma_start(out=t1_sb[:], in_=t_ones.rearrange("b x o -> x b o"))
             nc.scalar.dma_start(out=l1_sb[:], in_=lin1.rearrange("b x o -> x b o"))
             load_w(0)
-            load_tokens(x1, "x1", "tg", 4)
             load_w(1)
+            load_tokens(x1, "x1", "tg", 4)
             load_w(2)
             load_w(3)
             load_w(4)
@@ -285,7 +300,7 @@ def tile_biaffine_pa_kernel(tc, x1, x2, bw, W_bil, t_ones, lin1, lin2, b_lin, ou
             load_bias(0)
 
             make_identity(nc, ident[:])
-            nc.gpsimd.tensor_copy(out=identb[:], in_=ident[:])
+            nc.gpsimd.tensor_scalar(out=identb[:], in0=ident[:], scalar1=1.0, scalar2=0.0, op0=ALU.mult, op1=ALU.add)
             nc.gpsimd.memset(ecoef[:], 0.0)
 
             nc.vector.memset(warm[:], 0.0)
@@ -298,6 +313,18 @@ def tile_biaffine_pa_kernel(tc, x1, x2, bw, W_bil, t_ones, lin1, lin2, b_lin, ou
             nc.vector.tensor_scalar(out=nmax[:], in0=bmax[:], scalar1=-1.0, scalar2=None, op0=ALU.mult)
 
             nc.scalar.activation(out=bexp[:], in_=bwf[:], func=ACT.Exp, bias=nmax[:], scale=1.0)
+            transposes("x1", 1)
+            interleave_w(0, C_SPLIT0, G_SPLIT0)
+            quant_w(0)
+            grouped("x1", "tgx", 1)
+            copy_out("x1", nc.scalar.copy, [0])
+            copy_out("x1", nc.vector.tensor_copy, [1])
+            quant_tokens("x1", x1c[:], x1s[:])
+            stage1(0)
+            if rounds(1):
+                turn_w(1)
+            interleave_w(1, C_SPLIT1, G_SPLIT1)
+
             nc.vector.tensor_tensor(out=bsum[:], in0=bexp[:, 0:1], in1=bexp[:, 1:2], op=ALU.add)
             nc.vector.tensor_tensor(out=lsum[:], in0=l1_sb[:], in1=bl_sb[:].unsqueeze(1).to_broadcast([P, B, O]), op=ALU.add)
             nc.vector.reciprocal(out=brec[:], in_=bsum[:])
@@ -305,15 +332,6 @@ def tile_biaffine_pa_kernel(tc, x1, x2, bw, W_bil, t_ones, lin1, lin2, b_lin, ou
             nc.vector.tensor_scalar(out=lscl[:], in0=lsum[:].rearrange("p b o -> p (b o)"), scalar1=bwn[:, 1:2], scalar2=None, op0=ALU.mult)
             nc.vector.scalar_tensor_tensor(out=xterm[:], in0=t1_sb[:].rearrange("p b o -> p (b o)"), scalar=bwn[:, 0:1], in1=lscl[:], op0=ALU.mult, op1=ALU.add)
             rests[0] = (xterm, bwn[:, 1:2])
-
-            transposes("x1", 1)
-            interleave_w(0, C_SPLIT0, G_SPLIT0)
-            grouped("x1", "tgx", 1)
-            copy_out("x1", nc.vector.tensor_copy, [0, 1])
-            quant_w(0)
-            quant_tokens("x1", x1c[:], x1s[:])
-            stage1(0)
-            interleave_w(1, C_SPLIT, G_SPLIT)
 
             full = slice(0, L)
             for i in range(NP + 1):
@@ -328,7 +346,7 @@ def tile_biaffine_pa_kernel(tc, x1, x2, bw, W_bil, t_ones, lin1, lin2, b_lin, ou
                     load_lin2(i - L_STEP)
 
                 if i + 2 < NP and i <= EARLY:
-                    interleave_w(i + 2, C_SPLIT, G_SPLIT)
+                    interleave_w(i + 2, CS[rounds(i + 2)], CS[rounds(i + 2)])
                 v_words = [1, 3] if i > NP - TAIL else []
                 if i >= 1:
                     grouped(i - 1, "tg", 4)
@@ -341,14 +359,17 @@ def tile_biaffine_pa_kernel(tc, x1, x2, bw, W_bil, t_ones, lin1, lin2, b_lin, ou
 
                 if i >= LAG:
                     quant_t(i - LAG)
+                if i <= EA:
+                    add_bias(i)
+                    transposes(i, 2)
                 if i + 1 < NP:
                     quant_w(i + 1)
-                    if i + 2 < NP and i >= 1:
+                    if i + 2 < NP and rounds(i + 2):
                         turn_w(i + 2)
                     stage1(i + 1)
                 if v_words:
                     copy_out(i - 1, nc.vector.tensor_copy, v_words)
-                if i < NP:
+                if EA < i < NP:
                     add_bias(i)
                     transposes(i, 2)
                 if i == X2_STEP:
@@ -360,7 +381,7 @@ def tile_biaffine_pa_kernel(tc, x1, x2, bw, W_bil, t_ones, lin1, lin2, b_lin, ou
                 if i == X2_STEP + 3:
                     quant_tokens("x2", x2c[:], x2s[:])
                 if i + 2 < NP and i > EARLY:
-                    interleave_w(i + 2, C_SPLIT, G_SPLIT)
+                    interleave_w(i + 2, CS[rounds(i + 2)], CS[rounds(i + 2)])
                 if C_STEP <= i < C_STEP + TERMS:
                     split_ecoef(i - C_STEP)
 
@@ -371,12 +392,16 @@ def tile_biaffine_pa_kernel(tc, x1, x2, bw, W_bil, t_ones, lin1, lin2, b_lin, ou
             pair_bank(n)
             if n + LEAD < B * NG:
                 fill_e(n + LEAD)
-            if n < (B - 1) * NG:
-                mix(n, full)
-                if n % NG == NG - 1:
-                    nc.sync.dma_start(out=out[n // NG], in_=stages[n // NG][:])
-        for y0 in range(0, L, YH):
-            ysl = slice(y0, y0 + YH)
+            b, g = divmod(n, NG)
+            if b < B - 1:
+                mix(n, full if g < HOLD else slice(0, YH))
+                if g == NG - 1:
+                    nc.sync.dma_start(out=out[b, :, 0:YH, :], in_=stages[b][:, 0:YH, :])
+                    for m in range(n - NG + 1 + HOLD, n + 1):
+                        mix(m, slice(YH, L))
+                    nc.sync.dma_start(out=out[b, :, YH:, :], in_=stages[b][:, YH:, :])
+        for y0, y1 in Y_CUTS:
+            ysl = slice(y0, y1)
             for n in range((B - 1) * NG, B * NG):
                 mix(n, ysl)
             nc.sync.dma_start(out=out[B - 1, :, ysl, :], in_=stages[B - 1][:, ysl, :])

@@ -16,47 +16,37 @@ ACT = mybir.ActivationFunctionType
 
 P = 128
 PACK = 4
-OGRP = 4
-NG = O // OGRP
-YH = 64
-HOLD = 6
-Y_CUTS = ((0, 64), (64, 128))
-YE = L // NG
-RUN = 16
-TERMS = 3
-LROW = TERMS * O
-W_BUFS = 6
-C_SPLIT = 90
-G_SPLIT = 90
-C_SPLIT1 = 84
-G_SPLIT1 = 128
-C_SPLIT2 = 90
-G_SPLIT2 = 90
-ROUNDS = [0, 0, 1, 1, 1, 1, 1, 1, 1, 1, 1, 1, 1, 1, 1, 1]
-CS = [84, 88, 96]
-C_SPLIT0 = 64
-G_SPLIT0 = 128
-PE_GRP = 32
 OP = 2
 NP = O // OP
-X2_STEP = 4
-C_STEP = 2
-L_STEP = 7
-LEAD = 8
-W_GRP = 2
-EA = -1
-E_STEPS = 2
-EARLY = 1
-TAIL = 1
+OGRP = 4
+NG = O // OGRP
+RUN = 16
+YB = L // NG
+TERMS = 3
+LROW = TERMS * O
+
+PE_GRP = 32
+S_END = 92
+S_END_FIRST = (64, 84)
+
+W_BUFS = 6
+TG_BUFS = 4
 LAG = 3
-T_AT = {0: NP - 2, 3: NP - 1}
+AHEAD = NG
+E_STEPS = 2
+LAST_T = 3
+HOLD = 6
+YH = 64
+LOAD_X2, TURN_X2 = 2, 4
+SPLIT_E = 2
+LOAD_LIN2 = 7
 
 
 def tile_biaffine_pa_kernel(tc, x1, x2, bw, W_bil, t_ones, lin1, lin2, b_lin, out):
     nc = tc.nc
     with ExitStack() as ctx:
         keep = ctx.enter_context(tc.tile_pool(name="keep", bufs=1))
-        group = ctx.enter_context(tc.tile_pool(name="group", bufs=4))
+        group = ctx.enter_context(tc.tile_pool(name="group", bufs=TG_BUFS))
         psum = ctx.enter_context(tc.psum_pool(name="psum", bufs=8))
         ctx.enter_context(tc.manual_schedule())
 
@@ -76,7 +66,7 @@ def tile_biaffine_pa_kernel(tc, x1, x2, bw, W_bil, t_ones, lin1, lin2, b_lin, ou
         identb = keep.tile([P, P], BF16, name="identb", tag="identb")
         ecoef = keep.tile([P, B, P], BF16, name="ecoef", tag="ecoef", align_bytes=64)
         elhs = keep.tile([P, B, P], BF16, name="elhs", tag="elhs", align_bytes=64)
-        fold = keep.tile([P, O], F32, name="fold", tag="fold")
+        fold2 = keep.tile([P, O], F32, name="fold2", tag="fold2")
         fold3 = keep.tile([P, O], BF16, name="fold3", tag="fold3")
         erhs = keep.tile([P, L, O], BF16, name="erhs", tag="erhs", align_bytes=64)
         bwf = keep.tile([P, 2], F32, name="bwf", tag="bwf")
@@ -90,14 +80,14 @@ def tile_biaffine_pa_kernel(tc, x1, x2, bw, W_bil, t_ones, lin1, lin2, b_lin, ou
         lscl = keep.tile([P, B * O], F32, name="lscl", tag="lscl")
         xterm = keep.tile([P, B * O], F32, name="xterm", tag="xterm")
 
-        wraw, wgrp, wq, banks, tbs, xts, tgs, biases, exs, rests, stages, pairs, turned = {}, {}, {}, {}, {}, {}, {}, {}, {}, {}, {}, {}, {}
+        wraw, wgrp, wq, turned, banks, rows, xts, tgs, biases, rests, exs, stages, pairs = {}, {}, {}, {}, {}, {}, {}, {}, {}, {}, {}, {}, {}
 
         with tc.tile_pool(name="work", bufs=2) as work:
-            def load_tokens(x, key, tag, bufs):
-                raw = group.tile([P, B, D], BF16, name="xraw", tag=tag, bufs=bufs, align_bytes=64)
+            def load_tokens(x, key):
+                raw = group.tile([P, B, D], BF16, name="xraw", tag="tg", bufs=TG_BUFS, align_bytes=64)
                 for b in range(0, B, 2):
                     nc.sync.dma_start(out=raw[:, b : b + 2, :], in_=x[b : b + 2].rearrange("b x i -> x b i"))
-                tbs[key] = raw
+                rows[key] = raw
 
             def load_w(o):
                 raw = work.tile([P, PACK, D], BF16, name="wraw", tag="wraw", bufs=W_BUFS, align_bytes=64)
@@ -109,36 +99,33 @@ def tile_biaffine_pa_kernel(tc, x1, x2, bw, W_bil, t_ones, lin1, lin2, b_lin, ou
                 nc.sync.dma_start(out=bt[:], in_=W_bil[c * OGRP : (c + 1) * OGRP, D, :].partition_broadcast(P))
                 biases[c] = bt
 
-            def rounds(i):
-                return ROUNDS[i] if i < len(ROUNDS) else ROUNDS[-1]
-
             def turn_w(i):
-                turned[i] = []
-                for k in range(rounds(i)):
-                  wp = psum.tile([P, OP, PE_GRP * 4 * PACK], BF16, name="wp", tag="bank")
-                  for q in range(OP):
+                wp = psum.tile([P, OP, PE_GRP * 4 * PACK], BF16, name="wp", tag="bank")
+                for q in range(OP):
                     nc.tensor.matmul(
                         wp[:, q].rearrange("p (j h e) -> p h j e", h=2, e=2),
                         lhsT=identb[:],
-                        rhs=wraw[OP * i + q][:, :, k * PE_GRP * 4 : (k + 1) * PE_GRP * 4].rearrange("p (h e) j -> p h j e", e=2),
+                        rhs=wraw[OP * i + q][:, :, 0 : PE_GRP * 4].rearrange("p (h e) j -> p h j e", e=2),
                         start=True,
                         stop=True,
                     )
-                  turned[i].append(wp)
+                turned[i] = wp
 
-            def interleave_w(i, c_split, g_split):
-                g = work.tile([P, OP * D, PACK], BF16, name="wgrp", tag="wgrp", bufs=W_GRP, align_bytes=64)
+            def interleave_w(i):
+                g = work.tile([P, OP * D, PACK], BF16, name="wgrp", tag="wgrp", bufs=1, align_bytes=64)
+                first = i < len(S_END_FIRST)
+                lo = 0 if first else PE_GRP
+                hi = S_END_FIRST[i] if first else S_END
                 for q in range(OP):
                     dst = g[:].rearrange("p (q c t) s -> p q c s t", q=OP, t=4)[:, q]
                     src = wraw[OP * i + q][:].rearrange("p s (c t) -> p c s t", t=4)
-                    c0 = PE_GRP * len(turned.get(i, []))
-                    nc.scalar.copy(out=dst[:, c0:c_split], in_=src[:, c0:c_split])
-                    if c_split < g_split:
-                        nc.vector.tensor_copy(out=dst[:, c_split:g_split], in_=src[:, c_split:g_split])
-                    if g_split < P:
-                        nc.gpsimd.tensor_scalar(out=dst[:, g_split:], in0=src[:, g_split:], scalar1=1.0, scalar2=0.0, op0=ALU.mult, op1=ALU.add)
-                for k, wp in enumerate(turned.get(i, [])):
-                    nc.scalar.copy(out=g[:].rearrange("p (q j) s -> p q (j s)", q=OP)[:, :, k * PE_GRP * 16 : (k + 1) * PE_GRP * 16], in_=wp[:])
+                    nc.scalar.copy(out=dst[:, lo:hi], in_=src[:, lo:hi])
+                    if first:
+                        nc.vector.tensor_copy(out=dst[:, hi:], in_=src[:, hi:])
+                    else:
+                        nc.gpsimd.tensor_scalar(out=dst[:, hi:], in0=src[:, hi:], scalar1=1.0, scalar2=0.0, op0=ALU.mult, op1=ALU.add)
+                if not first:
+                    nc.scalar.copy(out=g[:].rearrange("p (q j) s -> p q (j s)", q=OP)[:, :, 0 : PE_GRP * 4 * PACK], in_=turned[i][:])
                 wgrp[i] = g
 
             def quant_w(i):
@@ -167,18 +154,18 @@ def tile_biaffine_pa_kernel(tc, x1, x2, bw, W_bil, t_ones, lin1, lin2, b_lin, ou
             def add_bias(i):
                 tb = work.tile([P, B, OP * D], BF16, name="tb", tag="tb", bufs=2, align_bytes=64)
                 per = OGRP // OP
-                rows = biases[i // per][:].rearrange("p g d -> p (g d)")[:, (i % per) * OP * D : (i % per + 1) * OP * D]
+                bias = biases[i // per][:].rearrange("p g d -> p (g d)")[:, (i % per) * OP * D : (i % per + 1) * OP * D]
                 for b in range(B):
                     nc.vector.tensor_tensor(
                         out=tb[:, b, :].rearrange("p (u a r) -> p a u r", u=2, r=RUN),
-                        in0=rows.rearrange("p (a u r) -> p a u r", u=2, r=RUN),
+                        in0=bias.rearrange("p (a u r) -> p a u r", u=2, r=RUN),
                         in1=banks[i][b][:].rearrange("p (a u r) -> p a u r", u=2, r=RUN),
                         op=ALU.add,
                     )
-                tbs[i] = tb
+                rows[i] = tb
 
             def transposes(key, n):
-                words = tbs[key][:].bitcast(F32)
+                words = rows[key][:].bitcast(F32)
                 xts[key] = []
                 for q in range(n):
                     for r in range(2):
@@ -194,13 +181,13 @@ def tile_biaffine_pa_kernel(tc, x1, x2, bw, W_bil, t_ones, lin1, lin2, b_lin, ou
                                 nc.tensor.transpose(xt[:, h, u, :], sel, ident[:])
                         xts[key].append(xt)
 
-            def grouped(key, tag, bufs):
+            def new_group(key, tag, bufs):
                 tgs[key] = group.tile([P, len(xts[key]) * 2 * L * PACK], BF16, name="tg", tag=tag, bufs=bufs, align_bytes=64)
 
-            def copy_out(key, copy, qs):
+            def copy_out(key, copy, which):
                 gw = tgs[key][:].bitcast(F32).rearrange("p (b x u) -> p b x u", x=L, u=2)
-                for q in qs:
-                    copy(out=gw[:, 2 * q : 2 * q + 2], in_=xts[key][q][:].rearrange("p h u x -> p h x u"))
+                for m in which:
+                    copy(out=gw[:, 2 * m : 2 * m + 2], in_=xts[key][m][:].rearrange("p h u x -> p h x u"))
 
             def quant_tokens(key, codes, scales):
                 nc.vector.quantize_mx(out=codes.bitcast(FP8X4), scales=scales, in_=tgs[key][:])
@@ -210,22 +197,24 @@ def tile_biaffine_pa_kernel(tc, x1, x2, bw, W_bil, t_ones, lin1, lin2, b_lin, ou
                 quant_tokens(i, tcod[:, osl, :].rearrange("p o n -> p (o n)"), tscl[:, osl, :].rearrange("p o n -> p (o n)"))
 
             def permute_x2():
-                x2p = group.tile([P, 2, B * D // 2], BF16, name="x2p", tag="tg", bufs=4, align_bytes=64)
+                x2p = group.tile([P, 2, B * D // 2], BF16, name="x2p", tag="tg", bufs=TG_BUFS, align_bytes=64)
                 nc.vector.tensor_copy(
                     out=x2p[:].rearrange("p u (n r) -> p n u r", r=RUN),
-                    in_=tbs["x2"][:].rearrange("p b (a u r) -> p (b a) u r", u=2, r=RUN),
+                    in_=rows["x2"][:].rearrange("p b (a u r) -> p (b a) u r", u=2, r=RUN),
                 )
-                tbs["x2"] = x2p
+                rows["x2"] = x2p
 
             def split_ecoef(t):
                 xrest, wrest = rests[t]
-                xt_out = ecoef[:, :, t * O : (t + 1) * O]
-                wt_out = ecoef[:].rearrange("p b k -> p (b k)")[:, LROW + t : LROW + t + (B - 1) * (P + TERMS) + 1 : P + TERMS]
-                nc.gpsimd.tensor_scalar(out=xt_out, in0=xrest[:].rearrange("p (b o) -> p b o", b=B), scalar1=1.0, scalar2=0.0, op0=ALU.mult, op1=ALU.add)
-                nc.gpsimd.tensor_scalar(out=wt_out, in0=wrest.to_broadcast([P, B]), scalar1=1.0, scalar2=0.0, op0=ALU.mult, op1=ALU.add)
+                x_out = ecoef[:, :, t * O : (t + 1) * O]
+                w_out = ecoef[:].rearrange("p b k -> p (b k)")[:, LROW + t : LROW + t + (B - 1) * (P + TERMS) + 1 : P + TERMS]
+                nc.gpsimd.tensor_scalar(out=x_out, in0=xrest[:].rearrange("p (b o) -> p b o", b=B), scalar1=1.0, scalar2=0.0, op0=ALU.mult, op1=ALU.add)
+                nc.gpsimd.tensor_scalar(out=w_out, in0=wrest.to_broadcast([P, B]), scalar1=1.0, scalar2=0.0, op0=ALU.mult, op1=ALU.add)
                 if t + 1 < TERMS:
                     xnext = keep.tile([P, B * O], F32, name="xrest%d" % t, tag="xrest%d" % t)
-                    nc.gpsimd.tensor_tensor(out=xnext[:].rearrange("p (b o) -> p b o", b=B), in0=xrest[:].rearrange("p (b o) -> p b o", b=B), in1=xt_out, op=ALU.subtract)
+                    nc.gpsimd.tensor_tensor(
+                        out=xnext[:].rearrange("p (b o) -> p b o", b=B), in0=xrest[:].rearrange("p (b o) -> p b o", b=B), in1=x_out, op=ALU.subtract
+                    )
                     wnext = keep.tile([P, 1], F32, name="wrest%d" % t, tag="wrest%d" % t)
                     nc.gpsimd.tensor_tensor(out=wnext[:], in0=wrest, in1=ecoef[:, 0, LROW + t : LROW + t + 1], op=ALU.subtract)
                     rests[t + 1] = (xnext, wnext[:])
@@ -245,12 +234,12 @@ def tile_biaffine_pa_kernel(tc, x1, x2, bw, W_bil, t_ones, lin1, lin2, b_lin, ou
             def fill_e(n):
                 b, c = divmod(n, NG)
                 if c == 0:
-                    if b:
-                        exs[b] = late.tile([P, L, O], F32, name="ex", tag="ex", bufs=2, align_bytes=64)
-                    else:
+                    if b == 0:
                         exs[b] = group.tile([P, L, O], F32, name="ex0", tag="ex0", bufs=1, align_bytes=64)
-                ysl = slice(c * YE, (c + 1) * YE)
-                eb = psum.tile([P, YE, O], F32, name="eb", tag="bank")
+                    else:
+                        exs[b] = late.tile([P, L, O], F32, name="ex", tag="ex", bufs=2, align_bytes=64)
+                ysl = slice(c * YB, (c + 1) * YB)
+                eb = psum.tile([P, YB, O], F32, name="eb", tag="bank")
                 nc.tensor.matmul(
                     eb[:].rearrange("p y o -> p (y o)"), lhsT=elhs[:, b, :], rhs=erhs[:, ysl, :].rearrange("p y o -> p (y o)"), start=True, stop=True
                 )
@@ -292,11 +281,9 @@ def tile_biaffine_pa_kernel(tc, x1, x2, bw, W_bil, t_ones, lin1, lin2, b_lin, ou
             nc.scalar.dma_start(out=l1_sb[:], in_=lin1.rearrange("b x o -> x b o"))
             load_w(0)
             load_w(1)
-            load_tokens(x1, "x1", "tg", 4)
-            load_w(2)
-            load_w(3)
-            load_w(4)
-            load_w(5)
+            load_tokens(x1, "x1")
+            for o in range(OP, W_BUFS):
+                load_w(o)
             load_bias(0)
 
             make_identity(nc, ident[:])
@@ -305,103 +292,99 @@ def tile_biaffine_pa_kernel(tc, x1, x2, bw, W_bil, t_ones, lin1, lin2, b_lin, ou
 
             nc.vector.memset(warm[:], 0.0)
             nc.scalar.activation(out=warm2[:], in_=warm[:], func=ACT.Exp)
-            nc.vector.tensor_tensor(out=fold[:], in0=ident[:, 0:O], in1=ident[:, O : 2 * O], op=ALU.add)
-            nc.vector.tensor_tensor(out=fold3[:], in0=fold[:], in1=ident[:, 2 * O : 3 * O], op=ALU.add)
+            nc.vector.tensor_tensor(out=fold2[:], in0=ident[:, 0:O], in1=ident[:, O : 2 * O], op=ALU.add)
+            nc.vector.tensor_tensor(out=fold3[:], in0=fold2[:], in1=ident[:, 2 * O : 3 * O], op=ALU.add)
             nc.vector.tensor_copy(out=erhs[:], in_=fold3[:].unsqueeze(1).to_broadcast([P, L, O]))
             nc.vector.tensor_copy(out=bwf[:], in_=bw_sb[:])
             nc.vector.tensor_tensor(out=bmax[:], in0=bwf[:, 0:1], in1=bwf[:, 1:2], op=ALU.max)
             nc.vector.tensor_scalar(out=nmax[:], in0=bmax[:], scalar1=-1.0, scalar2=None, op0=ALU.mult)
-
             nc.scalar.activation(out=bexp[:], in_=bwf[:], func=ACT.Exp, bias=nmax[:], scale=1.0)
+
             transposes("x1", 1)
-            interleave_w(0, C_SPLIT0, G_SPLIT0)
+            interleave_w(0)
             quant_w(0)
-            grouped("x1", "tgx", 1)
+            new_group("x1", "tgx", 1)
             copy_out("x1", nc.scalar.copy, [0])
             copy_out("x1", nc.vector.tensor_copy, [1])
             quant_tokens("x1", x1c[:], x1s[:])
             stage1(0)
-            if rounds(1):
-                turn_w(1)
-            interleave_w(1, C_SPLIT1, G_SPLIT1)
+            interleave_w(1)
 
             nc.vector.tensor_tensor(out=bsum[:], in0=bexp[:, 0:1], in1=bexp[:, 1:2], op=ALU.add)
             nc.vector.tensor_tensor(out=lsum[:], in0=l1_sb[:], in1=bl_sb[:].unsqueeze(1).to_broadcast([P, B, O]), op=ALU.add)
             nc.vector.reciprocal(out=brec[:], in_=bsum[:])
             nc.vector.tensor_scalar(out=bwn[:], in0=bexp[:], scalar1=brec[:], scalar2=None, op0=ALU.mult)
             nc.vector.tensor_scalar(out=lscl[:], in0=lsum[:].rearrange("p b o -> p (b o)"), scalar1=bwn[:, 1:2], scalar2=None, op0=ALU.mult)
-            nc.vector.scalar_tensor_tensor(out=xterm[:], in0=t1_sb[:].rearrange("p b o -> p (b o)"), scalar=bwn[:, 0:1], in1=lscl[:], op0=ALU.mult, op1=ALU.add)
+            nc.vector.scalar_tensor_tensor(
+                out=xterm[:], in0=t1_sb[:].rearrange("p b o -> p (b o)"), scalar=bwn[:, 0:1], in1=lscl[:], op0=ALU.mult, op1=ALU.add
+            )
             rests[0] = (xterm, bwn[:, 1:2])
 
-            full = slice(0, L)
             for i in range(NP + 1):
-                for o in (OP * (i + 3), OP * (i + 3) + 1):
-                    if o < O:
-                        load_w(o)
-                if i % 2 == 1 and i // 2 + 1 < O // OGRP:
+                for o in range(OP * (i + 3), min(OP * (i + 4), O)):
+                    load_w(o)
+                if i % 2 == 1 and i // 2 + 1 < NG:
                     load_bias(i // 2 + 1)
-                if i == X2_STEP - 2:
-                    load_tokens(x2, "x2", "tg", 4)
-                if L_STEP <= i < L_STEP + B:
-                    load_lin2(i - L_STEP)
+                if i == LOAD_X2:
+                    load_tokens(x2, "x2")
+                if LOAD_LIN2 <= i < LOAD_LIN2 + B:
+                    load_lin2(i - LOAD_LIN2)
 
-                if i + 2 < NP and i <= EARLY:
-                    interleave_w(i + 2, CS[rounds(i + 2)], CS[rounds(i + 2)])
-                v_words = [1, 3] if i > NP - TAIL else []
+                v_banks = [1, 3] if i == NP else []
                 if i >= 1:
-                    grouped(i - 1, "tg", 4)
-                    copy_out(i - 1, nc.scalar.copy, [q for q in range(4) if q not in v_words])
-                if i == C_STEP + TERMS + 1:
+                    new_group(i - 1, "tg", TG_BUFS)
+                    copy_out(i - 1, nc.scalar.copy, [m for m in range(4) if m not in v_banks])
+                if i == SPLIT_E + TERMS + 1:
                     turn_ecoef()
                 if NP - E_STEPS <= i < NP:
-                    for n in range((i - NP + E_STEPS) * LEAD // E_STEPS, (i - NP + E_STEPS + 1) * LEAD // E_STEPS):
+                    per = AHEAD // E_STEPS
+                    for n in range((i - NP + E_STEPS) * per, (i - NP + E_STEPS + 1) * per):
                         fill_e(n)
 
                 if i >= LAG:
                     quant_t(i - LAG)
-                if i <= EA:
-                    add_bias(i)
-                    transposes(i, 2)
                 if i + 1 < NP:
                     quant_w(i + 1)
-                    if i + 2 < NP and rounds(i + 2):
+                    if i + 2 < NP:
                         turn_w(i + 2)
                     stage1(i + 1)
-                if v_words:
-                    copy_out(i - 1, nc.vector.tensor_copy, v_words)
-                if EA < i < NP:
+                if v_banks:
+                    copy_out(i - 1, nc.vector.tensor_copy, v_banks)
+                if i < NP:
                     add_bias(i)
-                    transposes(i, 2)
-                if i == X2_STEP:
+                    transposes(i, OP)
+                if i == TURN_X2:
                     permute_x2()
                     transposes("x2", 1)
-                if i == X2_STEP + 1:
-                    grouped("x2", "tgx", 1)
+                if i == TURN_X2 + 1:
+                    new_group("x2", "tgx", 1)
                     copy_out("x2", nc.vector.tensor_copy, [0, 1])
-                if i == X2_STEP + 3:
+                if i == TURN_X2 + 3:
                     quant_tokens("x2", x2c[:], x2s[:])
-                if i + 2 < NP and i > EARLY:
-                    interleave_w(i + 2, CS[rounds(i + 2)], CS[rounds(i + 2)])
-                if C_STEP <= i < C_STEP + TERMS:
-                    split_ecoef(i - C_STEP)
+                if i + 2 < NP:
+                    interleave_w(i + 2)
+                if SPLIT_E <= i < SPLIT_E + TERMS:
+                    split_ecoef(i - SPLIT_E)
 
-        late = ctx.enter_context(tc.tile_pool(name="late", bufs=B))
+        late = ctx.enter_context(tc.tile_pool(name="late", bufs=3))
+        full, first_half, second_half = slice(0, L), slice(0, YH), slice(YH, L)
         for n in range(B * NG):
-            if n in T_AT:
-                quant_t(T_AT[n])
+            if n == 0:
+                quant_t(NP - 2)
+            if n == LAST_T:
+                quant_t(NP - 1)
             pair_bank(n)
-            if n + LEAD < B * NG:
-                fill_e(n + LEAD)
+            if n + AHEAD < B * NG:
+                fill_e(n + AHEAD)
             b, g = divmod(n, NG)
             if b < B - 1:
-                mix(n, full if g < HOLD else slice(0, YH))
+                mix(n, full if g < HOLD else first_half)
                 if g == NG - 1:
-                    nc.sync.dma_start(out=out[b, :, 0:YH, :], in_=stages[b][:, 0:YH, :])
+                    nc.sync.dma_start(out=out[b, :, first_half, :], in_=stages[b][:, first_half, :])
                     for m in range(n - NG + 1 + HOLD, n + 1):
-                        mix(m, slice(YH, L))
-                    nc.sync.dma_start(out=out[b, :, YH:, :], in_=stages[b][:, YH:, :])
-        for y0, y1 in Y_CUTS:
-            ysl = slice(y0, y1)
+                        mix(m, second_half)
+                    nc.sync.dma_start(out=out[b, :, second_half, :], in_=stages[b][:, second_half, :])
+        for ysl in (first_half, second_half):
             for n in range((B - 1) * NG, B * NG):
                 mix(n, ysl)
             nc.sync.dma_start(out=out[B - 1, :, ysl, :], in_=stages[B - 1][:, ysl, :])

from contextlib import ExitStack

import concourse.mybir as mybir
from concourse.masks import make_identity

B, L, D, O = 4, 128, 512, 32
FLOPS = 2 * B * L * D * D * O + 2 * O * B * L * L * D

F32 = mybir.dt.float32
BF16 = mybir.dt.bfloat16
U32 = mybir.dt.uint32
U8 = mybir.dt.uint8
FP8X4 = mybir.dt.float8_e4m3fn_x4
ALU = mybir.AluOpType
ACT = mybir.ActivationFunctionType

P = 128
PACK = 4
OP = 2
NP = O // OP
OGRP = 4
NG = O // OGRP
RUN = 16
YB = L // NG
TERMS = 3
LROW = TERMS * O

PE_GRP = 32
S_END = 92
S_END_FIRST = (64, 84)

W_BUFS = 6
TG_BUFS = 4
LAG = 3
AHEAD = NG
E_STEPS = 2
LAST_T = 3
HOLD = 6
YH = 64
LOAD_X2, TURN_X2 = 2, 4
SPLIT_E = 2
LOAD_LIN2 = 7


def tile_biaffine_pa_kernel(tc, x1, x2, bw, W_bil, t_ones, lin1, lin2, b_lin, out):
    nc = tc.nc
    with ExitStack() as ctx:
        keep = ctx.enter_context(tc.tile_pool(name="keep", bufs=1))
        group = ctx.enter_context(tc.tile_pool(name="group", bufs=TG_BUFS))
        psum = ctx.enter_context(tc.psum_pool(name="psum", bufs=8))
        ctx.enter_context(tc.manual_schedule())

        x1c = keep.tile([P, B * L], U32, name="x1c", tag="x1c", align_bytes=64)
        x1s = keep.tile([P, B * L], U8, name="x1s", tag="x1s", align_bytes=64)
        x2c = keep.tile([P, B * L], U32, name="x2c", tag="x2c", align_bytes=64)
        x2s = keep.tile([P, B * L], U8, name="x2s", tag="x2s", align_bytes=64)
        tcod = keep.tile([P, O, B * L], U32, name="tcod", tag="tcod", align_bytes=64)
        tscl = keep.tile([P, O, B * L], U8, name="tscl", tag="tscl", align_bytes=64)
        bw_sb = keep.tile([P, 2], BF16, name="bw_sb", tag="bw_sb")
        bl_sb = keep.tile([P, O], BF16, name="bl_sb", tag="bl_sb")
        t1_sb = keep.tile([P, B, O], BF16, name="t1_sb", tag="t1_sb")
        l1_sb = keep.tile([P, B, O], BF16, name="l1_sb", tag="l1_sb")
        warm = keep.tile([P, 1], F32, name="warm", tag="warm")
        warm2 = keep.tile([P, 1], F32, name="warm2", tag="warm2")
        ident = keep.tile([P, P], F32, name="ident", tag="ident")
        identb = keep.tile([P, P], BF16, name="identb", tag="identb")
        ecoef = keep.tile([P, B, P], BF16, name="ecoef", tag="ecoef", align_bytes=64)
        elhs = keep.tile([P, B, P], BF16, name="elhs", tag="elhs", align_bytes=64)
        fold2 = keep.tile([P, O], F32, name="fold2", tag="fold2")
        fold3 = keep.tile([P, O], BF16, name="fold3", tag="fold3")
        erhs = keep.tile([P, L, O], BF16, name="erhs", tag="erhs", align_bytes=64)
        bwf = keep.tile([P, 2], F32, name="bwf", tag="bwf")
        bmax = keep.tile([P, 1], F32, name="bmax", tag="bmax")
        nmax = keep.tile([P, 1], F32, name="nmax", tag="nmax")
        bexp = keep.tile([P, 2], F32, name="bexp", tag="bexp")
        bsum = keep.tile([P, 1], F32, name="bsum", tag="bsum")
        brec = keep.tile([P, 1], F32, name="brec", tag="brec")
        bwn = keep.tile([P, 2], F32, name="bwn", tag="bwn")
        lsum = keep.tile([P, B, O], F32, name="lsum", tag="lsum")
        lscl = keep.tile([P, B * O], F32, name="lscl", tag="lscl")
        xterm = keep.tile([P, B * O], F32, name="xterm", tag="xterm")

        wraw, wgrp, wq, turned, banks, rows, xts, tgs, biases, rests, exs, stages, pairs = {}, {}, {}, {}, {}, {}, {}, {}, {}, {}, {}, {}, {}

        with tc.tile_pool(name="work", bufs=2) as work:
            def load_tokens(x, key):
                raw = group.tile([P, B, D], BF16, name="xraw", tag="tg", bufs=TG_BUFS, align_bytes=64)
                for b in range(0, B, 2):
                    nc.sync.dma_start(out=raw[:, b : b + 2, :], in_=x[b : b + 2].rearrange("b x i -> x b i"))
                rows[key] = raw

            def load_w(o):
                raw = work.tile([P, PACK, D], BF16, name="wraw", tag="wraw", bufs=W_BUFS, align_bytes=64)
                nc.sync.dma_start(out=raw[:], in_=W_bil[o, 0:D, :].rearrange("(p s) j -> p s j", s=PACK))
                wraw[o] = raw

            def load_bias(c):
                bt = work.tile([P, OGRP, D], BF16, name="bias", tag="bias", bufs=2)
                nc.sync.dma_start(out=bt[:], in_=W_bil[c * OGRP : (c + 1) * OGRP, D, :].partition_broadcast(P))
                biases[c] = bt

            def turn_w(i):
                wp = psum.tile([P, OP, PE_GRP * 4 * PACK], BF16, name="wp", tag="bank")
                for q in range(OP):
                    nc.tensor.matmul(
                        wp[:, q].rearrange("p (j h e) -> p h j e", h=2, e=2),
                        lhsT=identb[:],
                        rhs=wraw[OP * i + q][:, :, 0 : PE_GRP * 4].rearrange("p (h e) j -> p h j e", e=2),
                        start=True,
                        stop=True,
                    )
                turned[i] = wp

            def interleave_w(i):
                g = work.tile([P, OP * D, PACK], BF16, name="wgrp", tag="wgrp", bufs=1, align_bytes=64)
                first = i < len(S_END_FIRST)
                lo = 0 if first else PE_GRP
                hi = S_END_FIRST[i] if first else S_END
                for q in range(OP):
                    dst = g[:].rearrange("p (q c t) s -> p q c s t", q=OP, t=4)[:, q]
                    src = wraw[OP * i + q][:].rearrange("p s (c t) -> p c s t", t=4)
                    nc.scalar.copy(out=dst[:, lo:hi], in_=src[:, lo:hi])
                    if first:
                        nc.vector.tensor_copy(out=dst[:, hi:], in_=src[:, hi:])
                    else:
                        nc.gpsimd.tensor_scalar(out=dst[:, hi:], in0=src[:, hi:], scalar1=1.0, scalar2=0.0, op0=ALU.mult, op1=ALU.add)
                if not first:
                    nc.scalar.copy(out=g[:].rearrange("p (q j) s -> p q (j s)", q=OP)[:, :, 0 : PE_GRP * 4 * PACK], in_=turned[i][:])
                wgrp[i] = g

            def quant_w(i):
                wc = work.tile([P, OP * D], U32, name="wc", tag="wc", bufs=2, align_bytes=64)
                ws = work.tile([P, OP * D], U8, name="ws", tag="ws", bufs=2, align_bytes=64)
                nc.vector.quantize_mx(out=wc[:].bitcast(FP8X4), scales=ws[:], in_=wgrp[i][:].rearrange("p j s -> p (j s)"))
                wq[i] = (wc, ws)

            def stage1(i):
                wc, ws = wq[i]
                banks[i] = []
                for b in range(B):
                    cols = slice(b * L, (b + 1) * L)
                    bank = psum.tile([P, OP * D], BF16, name="bank", tag="bank")
                    nc.tensor.matmul_mx(
                        out=bank[:],
                        lhsT=x1c[:, cols].bitcast(FP8X4),
                        lhsT_scale=x1s[:, cols],
                        rhs=wc[:].bitcast(FP8X4),
                        rhs_scale=ws[:],
                        start=True,
                        stop=True,
                    )
                    banks[i].append(bank)

            def add_bias(i):
                tb = work.tile([P, B, OP * D], BF16, name="tb", tag="tb", bufs=2, align_bytes=64)
                per = OGRP // OP
                bias = biases[i // per][:].rearrange("p g d -> p (g d)")[:, (i % per) * OP * D : (i % per + 1) * OP * D]
                for b in range(B):
                    nc.vector.tensor_tensor(
                        out=tb[:, b, :].rearrange("p (u a r) -> p a u r", u=2, r=RUN),
                        in0=bias.rearrange("p (a u r) -> p a u r", u=2, r=RUN),
                        in1=banks[i][b][:].rearrange("p (a u r) -> p a u r", u=2, r=RUN),
                        op=ALU.add,
                    )
                rows[i] = tb

            def transposes(key, n):
                words = rows[key][:].bitcast(F32)
                xts[key] = []
                for q in range(n):
                    for r in range(2):
                        xt = psum.tile([P, 2, 2, L], F32, name="xt", tag="bank")
                        for h in range(2):
                            for u in range(2):
                                if key == "x1":
                                    sel = words[:, 2 * r + h, u : D // 2 : 2]
                                elif key == "x2":
                                    sel = words[:, u, (2 * r + h) * P : (2 * r + h + 1) * P]
                                else:
                                    sel = words[:, 2 * r + h, (u * OP + q) * P : (u * OP + q + 1) * P]
                                nc.tensor.transpose(xt[:, h, u, :], sel, ident[:])
                        xts[key].append(xt)

            def new_group(key, tag, bufs):
                tgs[key] = group.tile([P, len(xts[key]) * 2 * L * PACK], BF16, name="tg", tag=tag, bufs=bufs, align_bytes=64)

            def copy_out(key, copy, which):
                gw = tgs[key][:].bitcast(F32).rearrange("p (b x u) -> p b x u", x=L, u=2)
                for m in which:
                    copy(out=gw[:, 2 * m : 2 * m + 2], in_=xts[key][m][:].rearrange("p h u x -> p h x u"))

            def quant_tokens(key, codes, scales):
                nc.vector.quantize_mx(out=codes.bitcast(FP8X4), scales=scales, in_=tgs[key][:])

            def quant_t(i):
                osl = slice(OP * i, OP * (i + 1))
                quant_tokens(i, tcod[:, osl, :].rearrange("p o n -> p (o n)"), tscl[:, osl, :].rearrange("p o n -> p (o n)"))

            def permute_x2():
                x2p = group.tile([P, 2, B * D // 2], BF16, name="x2p", tag="tg", bufs=TG_BUFS, align_bytes=64)
                nc.vector.tensor_copy(
                    out=x2p[:].rearrange("p u (n r) -> p n u r", r=RUN),
                    in_=rows["x2"][:].rearrange("p b (a u r) -> p (b a) u r", u=2, r=RUN),
                )
                rows["x2"] = x2p

            def split_ecoef(t):
                xrest, wrest = rests[t]
                x_out = ecoef[:, :, t * O : (t + 1) * O]
                w_out = ecoef[:].rearrange("p b k -> p (b k)")[:, LROW + t : LROW + t + (B - 1) * (P + TERMS) + 1 : P + TERMS]
                nc.gpsimd.tensor_scalar(out=x_out, in0=xrest[:].rearrange("p (b o) -> p b o", b=B), scalar1=1.0, scalar2=0.0, op0=ALU.mult, op1=ALU.add)
                nc.gpsimd.tensor_scalar(out=w_out, in0=wrest.to_broadcast([P, B]), scalar1=1.0, scalar2=0.0, op0=ALU.mult, op1=ALU.add)
                if t + 1 < TERMS:
                    xnext = keep.tile([P, B * O], F32, name="xrest%d" % t, tag="xrest%d" % t)
                    nc.gpsimd.tensor_tensor(
                        out=xnext[:].rearrange("p (b o) -> p b o", b=B), in0=xrest[:].rearrange("p (b o) -> p b o", b=B), in1=x_out, op=ALU.subtract
                    )
                    wnext = keep.tile([P, 1], F32, name="wrest%d" % t, tag="wrest%d" % t)
                    nc.gpsimd.tensor_tensor(out=wnext[:], in0=wrest, in1=ecoef[:, 0, LROW + t : LROW + t + 1], op=ALU.subtract)
                    rests[t + 1] = (xnext, wnext[:])

            def turn_ecoef():
                et = psum.tile([P, B, P], BF16, name="et", tag="bank")
                for b in range(B):
                    nc.tensor.transpose(et[:, b, :], ecoef[:, b, :], identb[:])
                nc.scalar.copy(out=elhs[:], in_=et[:])

            def load_lin2(b):
                nc.sync.dma_start(
                    out=erhs[LROW + TERMS * b : LROW + TERMS * (b + 1)].rearrange("p y o -> p (y o)"),
                    in_=lin2[b].rearrange("y o -> (y o)").partition_broadcast(TERMS),
                )

            def fill_e(n):
                b, c = divmod(n, NG)
                if c == 0:
                    if b == 0:
                        exs[b] = group.tile([P, L, O], F32, name="ex0", tag="ex0", bufs=1, align_bytes=64)
                    else:
                        exs[b] = late.tile([P, L, O], F32, name="ex", tag="ex", bufs=2, align_bytes=64)
                ysl = slice(c * YB, (c + 1) * YB)
                eb = psum.tile([P, YB, O], F32, name="eb", tag="bank")
                nc.tensor.matmul(
                    eb[:].rearrange("p y o -> p (y o)"), lhsT=elhs[:, b, :], rhs=erhs[:, ysl, :].rearrange("p y o -> p (y o)"), start=True, stop=True
                )
                nc.scalar.copy(out=exs[b][:, ysl, :], in_=eb[:])

            def pair_bank(n):
                b, g = divmod(n, NG)
                cols = slice(b * L, (b + 1) * L)
                pb = psum.tile([P, OGRP, L], F32, name="pair", tag="bank")
                for k in range(OGRP):
                    o = g * OGRP + k
                    nc.tensor.matmul_mx(
                        out=pb[:, k, :],
                        lhsT=tcod[:, o, cols].bitcast(FP8X4),
                        lhsT_scale=tscl[:, o, cols],
                        rhs=x2c[:, cols].bitcast(FP8X4),
                        rhs_scale=x2s[:, cols],
                        start=True,
                        stop=True,
                    )
                pairs[n] = pb

            def mix(n, ysl):
                b, g = divmod(n, NG)
                if b not in stages:
                    stages[b] = late.tile([P, L, O], F32, name="stage", tag="stage", bufs=3, align_bytes=64)
                nc.vector.scalar_tensor_tensor(
                    out=stages[b][:, ysl, g * OGRP : (g + 1) * OGRP],
                    in0=pairs[n][:, :, ysl].rearrange("p k y -> p y k"),
                    scalar=bwn[:, 0:1],
                    in1=exs[b][:, ysl, g * OGRP : (g + 1) * OGRP],
                    op0=ALU.mult,
                    op1=ALU.add,
                )

            nc.scalar.dma_start(out=bw_sb[:], in_=bw.partition_broadcast(P))
            nc.scalar.dma_start(out=bl_sb[:], in_=b_lin.partition_broadcast(P))
            nc.scalar.dma_start(out=t1_sb[:], in_=t_ones.rearrange("b x o -> x b o"))
            nc.scalar.dma_start(out=l1_sb[:], in_=lin1.rearrange("b x o -> x b o"))
            load_w(0)
            load_w(1)
            load_tokens(x1, "x1")
            for o in range(OP, W_BUFS):
                load_w(o)
            load_bias(0)

            make_identity(nc, ident[:])
            nc.gpsimd.tensor_scalar(out=identb[:], in0=ident[:], scalar1=1.0, scalar2=0.0, op0=ALU.mult, op1=ALU.add)
            nc.gpsimd.memset(ecoef[:], 0.0)

            nc.vector.memset(warm[:], 0.0)
            nc.scalar.activation(out=warm2[:], in_=warm[:], func=ACT.Exp)
            nc.vector.tensor_tensor(out=fold2[:], in0=ident[:, 0:O], in1=ident[:, O : 2 * O], op=ALU.add)
            nc.vector.tensor_tensor(out=fold3[:], in0=fold2[:], in1=ident[:, 2 * O : 3 * O], op=ALU.add)
            nc.vector.tensor_copy(out=erhs[:], in_=fold3[:].unsqueeze(1).to_broadcast([P, L, O]))
            nc.vector.tensor_copy(out=bwf[:], in_=bw_sb[:])
            nc.vector.tensor_tensor(out=bmax[:], in0=bwf[:, 0:1], in1=bwf[:, 1:2], op=ALU.max)
            nc.vector.tensor_scalar(out=nmax[:], in0=bmax[:], scalar1=-1.0, scalar2=None, op0=ALU.mult)
            nc.scalar.activation(out=bexp[:], in_=bwf[:], func=ACT.Exp, bias=nmax[:], scale=1.0)

            transposes("x1", 1)
            interleave_w(0)
            quant_w(0)
            new_group("x1", "tgx", 1)
            copy_out("x1", nc.scalar.copy, [0])
            copy_out("x1", nc.vector.tensor_copy, [1])
            quant_tokens("x1", x1c[:], x1s[:])
            stage1(0)
            interleave_w(1)

            nc.vector.tensor_tensor(out=bsum[:], in0=bexp[:, 0:1], in1=bexp[:, 1:2], op=ALU.add)
            nc.vector.tensor_tensor(out=lsum[:], in0=l1_sb[:], in1=bl_sb[:].unsqueeze(1).to_broadcast([P, B, O]), op=ALU.add)
            nc.vector.reciprocal(out=brec[:], in_=bsum[:])
            nc.vector.tensor_scalar(out=bwn[:], in0=bexp[:], scalar1=brec[:], scalar2=None, op0=ALU.mult)
            nc.vector.tensor_scalar(out=lscl[:], in0=lsum[:].rearrange("p b o -> p (b o)"), scalar1=bwn[:, 1:2], scalar2=None, op0=ALU.mult)
            nc.vector.scalar_tensor_tensor(
                out=xterm[:], in0=t1_sb[:].rearrange("p b o -> p (b o)"), scalar=bwn[:, 0:1], in1=lscl[:], op0=ALU.mult, op1=ALU.add
            )
            rests[0] = (xterm, bwn[:, 1:2])

            for i in range(NP + 1):
                for o in range(OP * (i + 3), min(OP * (i + 4), O)):
                    load_w(o)
                if i % 2 == 1 and i // 2 + 1 < NG:
                    load_bias(i // 2 + 1)
                if i == LOAD_X2:
                    load_tokens(x2, "x2")
                if LOAD_LIN2 <= i < LOAD_LIN2 + B:
                    load_lin2(i - LOAD_LIN2)

                v_banks = [1, 3] if i == NP else []
                if i >= 1:
                    new_group(i - 1, "tg", TG_BUFS)
                    copy_out(i - 1, nc.scalar.copy, [m for m in range(4) if m not in v_banks])
                if i == SPLIT_E + TERMS + 1:
                    turn_ecoef()
                if NP - E_STEPS <= i < NP:
                    per = AHEAD // E_STEPS
                    for n in range((i - NP + E_STEPS) * per, (i - NP + E_STEPS + 1) * per):
                        fill_e(n)

                if i >= LAG:
                    quant_t(i - LAG)
                if i + 1 < NP:
                    quant_w(i + 1)
                    if i + 2 < NP:
                        turn_w(i + 2)
                    stage1(i + 1)
                if v_banks:
                    copy_out(i - 1, nc.vector.tensor_copy, v_banks)
                if i < NP:
                    add_bias(i)
                    transposes(i, OP)
                if i == TURN_X2:
                    permute_x2()
                    transposes("x2", 1)
                if i == TURN_X2 + 1:
                    new_group("x2", "tgx", 1)
                    copy_out("x2", nc.vector.tensor_copy, [0, 1])
                if i == TURN_X2 + 3:
                    quant_tokens("x2", x2c[:], x2s[:])
                if i + 2 < NP:
                    interleave_w(i + 2)
                if SPLIT_E <= i < SPLIT_E + TERMS:
                    split_ecoef(i - SPLIT_E)

        late = ctx.enter_context(tc.tile_pool(name="late", bufs=3))
        full, first_half, second_half = slice(0, L), slice(0, YH), slice(YH, L)
        for n in range(B * NG):
            if n == 0:
                quant_t(NP - 2)
            if n == LAST_T:
                quant_t(NP - 1)
            pair_bank(n)
            if n + AHEAD < B * NG:
                fill_e(n + AHEAD)
            b, g = divmod(n, NG)
            if b < B - 1:
                mix(n, full if g < HOLD else first_half)
                if g == NG - 1:
                    nc.sync.dma_start(out=out[b, :, first_half, :], in_=stages[b][:, first_half, :])
                    for m in range(n - NG + 1 + HOLD, n + 1):
                        mix(m, second_half)
                    nc.sync.dma_start(out=out[b, :, second_half, :], in_=stages[b][:, second_half, :])
        for ysl in (first_half, second_half):
            for n in range((B - 1) * NG, B * NG):
                mix(n, ysl)
            nc.sync.dma_start(out=out[B - 1, :, ysl, :], in_=stages[B - 1][:, ysl, :])
